import numpy as np
import ml_dtypes


def mxq(x, axis, fmt="e4m3"):
    dtype, down = {"e4m3": (ml_dtypes.float8_e4m3fn, 7), "e5m2": (ml_dtypes.float8_e5m2, 14)}[fmt]
    v = np.moveaxis(np.asarray(x, np.float32).astype(ml_dtypes.bfloat16).astype(np.float64), axis, -1)
    blocks = v.reshape(v.shape[:-1] + (-1, 32))
    amax = np.abs(blocks).max(-1, keepdims=True)
    byte = np.maximum(np.where(amax > 0, np.frexp(amax)[1] - 1 + 127, 0) - down, 1)
    scale = np.exp2(byte - 127.0)
    codes = (blocks / scale).astype(np.float32).astype(dtype).astype(np.float64)
    return np.moveaxis((codes * scale).reshape(v.shape), -1, axis)


WIDE = False


def mx_kscale(k):
    if not WIDE:
        return np.ones(k)
    levels = np.array([10, -10, 5, -5, 0])
    a = np.random.permutation(np.resize(levels, k // 512 * 4)).reshape(k // 512, 4)
    idx = np.arange(k)
    return np.exp2(a[idx // 512, idx % 128 // 32])


BF16 = ml_dtypes.bfloat16


def bf(x):
    return np.asarray(x, np.float32).astype(BF16)


def f64(x):
    return np.asarray(x).astype(np.float64)


NQ, NK, QS, KS, F, DEG = 1024, 1024, 512, 512, 512, 32
EPS = 1e-5
SLOPE = 0.01


def leaky(v):
    return np.where(v >= 0, v, SLOPE * v)


def setup_inputs():
    s, t = mx_kscale(QS), mx_kscale(F)
    return {"x": bf(np.random.standard_normal((NQ, QS)) * s),
            "w1": bf(np.random.standard_normal((QS, F)) / np.sqrt(QS) / s[:, None] * t),
            "b1": bf(np.random.standard_normal(F) * 0.5 * t),
            "w2": bf(np.random.standard_normal((F, F)) / np.sqrt(F) / t[:, None]),
            "b2": bf(np.random.standard_normal(F) * 0.5),
            "gamma": bf(1.0 + 0.1 * np.random.standard_normal(F)),
            "beta": bf(0.1 * np.random.standard_normal(F))}


def reference(x, w1, b1, w2, b2, gamma, beta):
    h = leaky((mxq(f64(x), 1, "e4m3") @ mxq(f64(w1), 0, "e4m3")) + f64(b1))
    h = leaky((mxq(h, 1, "e4m3") @ mxq(f64(w2), 0, "e4m3")) + f64(b2))
    mean = h.mean(axis=0)
    var = h.var(axis=0)
    return f64(gamma) * (h - mean) / np.sqrt(var + EPS) + f64(beta)

@@ -1,0 +1,312 @@
+from contextlib import ExitStack
+
+import concourse.mybir as mybir
+from concourse.masks import make_identity
+
+F32 = mybir.dt.float32
+BF16 = mybir.dt.bfloat16
+U32 = mybir.dt.uint32
+U8 = mybir.dt.uint8
+FP8X4 = mybir.dt.float8_e4m3fn_x4
+ALU = mybir.AluOpType
+ACT = mybir.ActivationFunctionType
+
+P = 128
+NQ = 1024
+K = 512
+F = 512
+EPS = 1e-5
+SLOPE = 0.01
+FLOPS = 2 * NQ * K * F * 2
+
+STAT = ["V","V","V","V"]
+NORM = [["G","G"],["G","G"],["G","G"],["V","G"]]
+EVAC = [["S","S"],["S","S"],["S","S"],["S","V"]]
+SCHED = (
+    ("vf1",), ("vT1",), ("rg", "w1a", "V"), ("xT", 0), ("vc1",), ("qw", "w1a"),
+    ("rg", "w1b", "V"), ("xc", 0, "S"), ("xT", 1), ("qw", "w1b"), ("xq", 0), ("xT", 2),
+    ("xc", 1, "S"), ("m1", 0), ("xc", 2, "S"), ("xq", 1), ("xT", 3), ("s1", 0, 0),
+    ("xq", 2), ("m1", 1), ("s1", 0, 1), ("rg", "w2", "V"), ("s1", 0, 2), ("m1", 2),
+    ("s1", 0, 3), ("s1", 1, 0), ("lk", 0), ("s1", 1, 1), ("s1", 1, 2), ("s1", 1, 3),
+    ("xc", 3, "S"), ("hq", 0), ("lk", 1), ("vf2",), ("s1", 2, 0), ("vT2",),
+    ("s1", 2, 1), ("vc2",), ("hq", 1), ("s1", 2, 2), ("xq", 3), ("s1", 2, 3),
+    ("qw", "w2"), ("m1", 3), ("lk", 2), ("s1", 3, 0), ("m2", 0, 0), ("s1", 3, 1),
+    ("m2", 1, 0), ("s1", 3, 2), ("s1", 3, 3), ("hq", 2), ("a0", 0, 0), ("lk", 3),
+    ("a0", 1, 0), ("hq", 3), ("st", 0, 0), ("m2", 0, 1), ("m2", 1, 1), ("bn", 0, 0),
+    ("a0", 0, 1), ("m2", 2, 0), ("st", 1, 0), ("a0", 1, 1), ("a0", 2, 0), ("st", 0, 1),
+    ("m2", 3, 0), ("bn", 0, 1), ("a0", 3, 0), ("m2", 2, 1), ("ag", 0), ("a0", 2, 1),
+    ("bn", 1, 0), ("rs", 0), ("st", 1, 1), ("ab", 0), ("m2", 3, 1), ("bn", 1, 1),
+    ("nm", 0, 0), ("a0", 3, 1), ("ag", 1), ("st", 2, 0), ("nm", 0, 1), ("oT", 0, 0),
+    ("rs", 1), ("bn", 2, 0), ("ev", 0, 0), ("oT", 0, 1), ("ab", 1), ("st", 2, 1),
+    ("ev", 0, 1), ("nm", 1, 0), ("bn", 2, 1), ("nm", 1, 1), ("oT", 1, 0), ("ag", 2),
+    ("st", 3, 0), ("rs", 2), ("oT", 1, 1), ("ev", 1, 0), ("ab", 2), ("bn", 3, 0),
+    ("ev", 1, 1), ("nm", 2, 0), ("st", 3, 1), ("nm", 2, 1), ("oT", 2, 0), ("bn", 3, 1),
+    ("ev", 2, 0), ("oT", 2, 1), ("ag", 3), ("rs", 3), ("ev", 2, 1), ("ab", 3),
+    ("nm", 3, 0), ("nm", 3, 1), ("oT", 3, 0), ("oT", 3, 1), ("ev", 3, 0), ("ev", 3, 1),
+)
+
+
+def tile_attention_prop_pa_kernel(tc, x, w1, b1, w2, b2, gamma, beta, out):
+    nc = tc.nc
+    with ExitStack() as ctx:
+        keep = ctx.enter_context(tc.tile_pool(name="keep", bufs=1))
+        ps = ctx.enter_context(tc.psum_pool(name="ps", bufs=4))
+        ctx.enter_context(tc.manual_schedule())
+        T = {}
+
+        vb1 = keep.tile([P, P], BF16, name="vb1")
+        nc.vector.memset(vb1[:], 0.0)
+        vr = keep.tile([P, P], BF16, name="vr")
+        nc.vector.memset(vr[:], 0.0)
+        one = keep.tile([P, 1], F32, name="one")
+        nc.vector.memset(one[:], 1.0)
+        nc.scalar.dma_start(out=vb1[0:4, :], in_=b1.rearrange("(t p) -> t p", p=P))
+        warm = keep.tile([P, 1], F32, name="warm")
+        nc.scalar.activation(out=warm[:], in_=one[:], func=ACT.Abs_reciprocal_sqrt)
+        ident = keep.tile([P, P], F32, name="ident")
+        make_identity(nc, ident[:])
+        for r, vec in enumerate((b2, gamma, beta)):
+            nc.gpsimd.dma_start(out=vr[4 * r : 4 * r + 4, :], in_=vec.rearrange("(t p) -> t p", p=P))
+
+        w1_view = w1.rearrange("(p j) f -> p j f", j=4)
+        x_view = x.rearrange("(i c) k -> i (c k)", c=8)
+        wsb = {}
+        x_sb = {}
+
+        def load_w1(nm, lo):
+            wsb[nm] = keep.tile([P, 4, 256], BF16, name="sb_" + nm)
+            nc.sync.dma_start(out=wsb[nm][:], in_=w1_view[:, :, lo : lo + 256])
+
+        def load_x(j):
+            x_sb[j] = keep.tile([P, 1024], BF16, name="x_sb%d" % j)
+            nc.sync.dma_start(out=x_sb[j][:], in_=x_view[:, 1024 * j : 1024 * (j + 1)])
+
+        load_w1("w1a", 0)
+        load_x(0)
+        load_w1("w1b", 256)
+        load_x(1)
+        load_x(2)
+        load_x(3)
+        wsb["w2"] = keep.tile([P, 4, F], BF16, name="sb_w2")
+        nc.sync.dma_start(out=wsb["w2"][:], in_=w2.rearrange("(t p) f -> p t f", p=P))
+
+        w1q = keep.tile([P, F], U32, align_bytes=64, name="w1q")
+        w1s = keep.tile([P, F], U8, align_bytes=64, name="w1s")
+        w2q = keep.tile([P, F], U32, align_bytes=64, name="w2q")
+        w2s = keep.tile([P, F], U8, align_bytes=64, name="w2s")
+        xq = keep.tile([P, NQ], U32, align_bytes=64, name="xq")
+        xs = keep.tile([P, NQ], U8, align_bytes=64, name="xs")
+        hq = keep.tile([P, NQ], U32, align_bytes=64, name="hq")
+        hs = keep.tile([P, NQ], U8, align_bytes=64, name="hs")
+        wdst = {"w1a": (w1q, w1s, 0, 256), "w1b": (w1q, w1s, 256, 256), "w2": (w2q, w2s, 0, 512)}
+        b1T = keep.tile([P, 4], F32, name="b1T")
+        rT = keep.tile([P, 12], F32, name="rT")
+        b2s = keep.tile([P, 4], F32, name="b2s")
+        gpair = keep.tile([P, 4, 2], F32, name="gpair")
+        out_view = out.rearrange("(i c) f -> i c f", c=8)
+
+        def step(tok):
+            k = tok[0]
+            if k == "vf1":
+                T["vf1"] = keep.tile([P, P], F32, name="vf1")
+                nc.vector.tensor_copy(out=T["vf1"][:], in_=vb1[:])
+            elif k == "vT1":
+                T["vp1"] = ps.tile([P, P], F32, tag="tr", name="vp1")
+                nc.tensor.transpose(T["vp1"][:], T["vf1"][:], ident[:])
+            elif k == "vc1":
+                nc.vector.tensor_copy(out=b1T[:], in_=T["vp1"][:, 0:4])
+            elif k == "vf2":
+                T["vf2"] = keep.tile([P, P], F32, name="vf2")
+                nc.scalar.copy(out=T["vf2"][:], in_=vr[:])
+            elif k == "vT2":
+                T["vp2"] = ps.tile([P, P], F32, tag="tr", name="vp2")
+                nc.tensor.transpose(T["vp2"][:], T["vf2"][:], ident[:])
+            elif k == "vc2":
+                nc.scalar.copy(out=rT[:], in_=T["vp2"][:, 0:12])
+                nc.scalar.mul(out=b2s[:], in_=rT[:, 0:4], mul=1.0 - SLOPE)
+                nc.scalar.copy(out=gpair[:, :, 0], in_=rT[:, 4:8])
+                nc.scalar.mul(out=gpair[:, :, 1], in_=rT[:, 4:8], mul=-1.0)
+            elif k == "rg":
+                nm = tok[1]
+                width = wdst[nm][3]
+                g = keep.tile([P, width, 4], BF16, align_bytes=64, name="g_" + nm)
+                T["g_" + nm] = g
+                dst = g[:].rearrange("p (c i) t -> p c t i", i=4)
+                src = wsb[nm][:].rearrange("p t (c i) -> p c t i", i=4)
+                if tok[2] == "V":
+                    nc.vector.tensor_copy(out=dst, in_=src)
+                else:
+                    nc.scalar.copy(out=dst, in_=src)
+            elif k == "qw":
+                nm = tok[1]
+                codes, scales, lo, width = wdst[nm]
+                nc.vector.quantize_mx(
+                    out=codes[:, lo : lo + width].bitcast(FP8X4),
+                    scales=scales[:, lo : lo + width],
+                    in_=T["g_" + nm][:].rearrange("p f t -> p (f t)"),
+                )
+            elif k == "xT":
+                j = tok[1]
+                xt = ps.tile([P, 2, 2, P], F32, tag="tr", name="xt%d" % j)
+                T["xt", j] = xt
+                xw = x_sb[j][:].bitcast(F32).rearrange("i (cc w u) -> i cc u w", cc=2, u=2)
+                for cc in range(2):
+                    for u in range(2):
+                        nc.tensor.transpose(xt[:, cc, u, :], xw[:, cc, u, :], ident[:])
+            elif k == "xc":
+                j = tok[1]
+                xg = keep.tile([P, 1024], BF16, align_bytes=64, name="xg%d" % j)
+                T["xg", j] = xg
+                dst = xg[:].bitcast(F32).rearrange("p (cc i u) -> p cc i u", cc=2, u=2)
+                src = T["xt", j][:].rearrange("p cc u i -> p cc i u")
+                if tok[2] == "S":
+                    nc.scalar.copy(out=dst, in_=src)
+                else:
+                    nc.vector.tensor_copy(out=dst, in_=src)
+            elif k == "xq":
+                j = tok[1]
+                sl = slice(256 * j, 256 * (j + 1))
+                nc.vector.quantize_mx(out=xq[:, sl].bitcast(FP8X4), scales=xs[:, sl], in_=T["xg", j][:])
+            elif k == "m1":
+                pi = tok[1]
+                sl = slice(256 * pi, 256 * (pi + 1))
+                T["v", pi] = keep.tile([P, 4, 256], F32, name="v%d" % pi)
+                for tp in range(2):
+                    bank = ps.tile([P, 2, 256], F32, tag="mm", name="l1_%d_%d" % (pi, tp))
+                    T["l1", pi, tp] = bank
+                    for e in range(2):
+                        t = 2 * tp + e
+                        nc.tensor.matmul_mx(
+                            out=bank[:, e, :],
+                            lhsT=w1q[:, P * t : P * (t + 1)].bitcast(FP8X4),
+                            lhsT_scale=w1s[:, P * t : P * (t + 1)],
+                            rhs=xq[:, sl].bitcast(FP8X4),
+                            rhs_scale=xs[:, sl],
+                            start=True,
+                            stop=True,
+                        )
+            elif k == "s1":
+                pi, t = tok[1], tok[2]
+                nc.scalar.activation(
+                    out=T["v", pi][:, t, :],
+                    in_=T["l1", pi, t // 2][:, t % 2, :],
+                    func=ACT.Identity,
+                    bias=b1T[:, t : t + 1],
+                    scale=1.0,
+                )
+            elif k == "lk":
+                pi = tok[1]
+                hg = keep.tile([P, 256, 4], BF16, align_bytes=64, name="hg%d" % pi)
+                T["hg", pi] = hg
+                vp = T["v", pi][:].rearrange("p t n -> p n t")
+                nc.vector.scalar_tensor_tensor(out=hg[:], in0=vp, scalar=SLOPE, in1=vp, op0=ALU.mult, op1=ALU.max)
+            elif k == "hq":
+                pi = tok[1]
+                sl = slice(256 * pi, 256 * (pi + 1))
+                nc.vector.quantize_mx(
+                    out=hq[:, sl].bitcast(FP8X4), scales=hs[:, sl], in_=T["hg", pi][:].rearrange("p n t -> p (n t)")
+                )
+            elif k == "m2":
+                c, h = tok[1], tok[2]
+                fs = slice(P * c, P * (c + 1))
+                cols = slice(512 * h, 512 * (h + 1))
+                p2 = ps.tile([P, 512], F32, tag="mm", name="l2_%d_%d" % (c, h))
+                T["l2", c, h] = p2
+                nc.tensor.matmul_mx(
+                    out=p2[:],
+                    lhsT=w2q[:, fs].bitcast(FP8X4),
+                    lhsT_scale=w2s[:, fs],
+                    rhs=hq[:, cols].bitcast(FP8X4),
+                    rhs_scale=hs[:, cols],
+                    start=True,
+                    stop=True,
+                )
+            elif k == "a0":
+                c, h = tok[1], tok[2]
+                T["a0", c, h] = keep.tile([P, 512], F32, name="a0_%d_%d" % (c, h))
+                nc.scalar.mul(out=T["a0", c, h][:], in_=T["l2", c, h][:], mul=SLOPE)
+            elif k == "st":
+                c, h = tok[1], tok[2]
+                if h == 0:
+                    T["q", c] = keep.tile([P, NQ], F32, name="q%d" % c)
+                    T["stats", c] = keep.tile([P, 2, 6], F32, name="stats%d" % c)
+                nc.vector.scalar_tensor_tensor(
+                    out=T["q", c][:, 512 * h : 512 * (h + 1)],
+                    in0=T["l2", c, h][:],
+                    scalar=b2s[:, c : c + 1],
+                    in1=T["a0", c, h][:],
+                    op0=ALU.add,
+                    op1=ALU.max,
+                )
+            elif k == "bn":
+                c, h = tok[1], tok[2]
+                nc.vector.bn_stats(out=T["stats", c][:, h, :], in_=T["q", c][:, 512 * h : 512 * (h + 1)])
+            elif k == "ag":
+                c = tok[1]
+                T["mv", c] = keep.tile([P, 2], F32, name="mv%d" % c)
+                nc.vector.bn_aggr(out=T["mv", c][:], in_=T["stats", c][:].rearrange("p a b -> p (a b)"))
+            elif k == "rs":
+                c = tok[1]
+                T["rstd", c] = keep.tile([P, 1], F32, name="rstd%d" % c)
+                nc.scalar.activation(
+                    out=T["rstd", c][:], in_=T["mv", c][:, 1:2], func=ACT.Abs_reciprocal_sqrt, bias=EPS, scale=1.0
+                )
+            elif k == "ab":
+                c = tok[1]
+                T["ab", c] = keep.tile([P, 2], F32, name="ab%d" % c)
+                T["sh", c] = keep.tile([P, 1], F32, name="sh%d" % c)
+                nc.vector.tensor_scalar(
+                    out=T["ab", c][:], in0=gpair[:, c, :], scalar1=T["rstd", c][:, 0:1], scalar2=None, op0=ALU.mult
+                )
+                nc.vector.scalar_tensor_tensor(
+                    out=T["sh", c][:],
+                    in0=T["mv", c][:, 0:1],
+                    scalar=T["ab", c][:, 1:2],
+                    in1=rT[:, 8 + c : 9 + c],
+                    op0=ALU.mult,
+                    op1=ALU.add,
+                )
+            elif k == "nm":
+                c, h = tok[1], tok[2]
+                if h == 0:
+                    T["y", c] = keep.tile([P, NQ], F32, name="y%d" % c)
+                cols = slice(512 * h, 512 * (h + 1))
+                eng = NORM[c][h]
+                if eng == "S":
+                    nc.scalar.activation(
+                        out=T["y", c][:, cols],
+                        in_=T["q", c][:, cols],
+                        func=ACT.Identity,
+                        bias=T["sh", c][:, 0:1],
+                        scale=T["ab", c][:, 0:1],
+                    )
+                else:
+                    e = nc.gpsimd if eng == "G" else nc.vector
+                    e.tensor_scalar(
+                        out=T["y", c][:, cols],
+                        in0=T["q", c][:, cols],
+                        scalar1=T["ab", c][:, 0:1],
+                        scalar2=T["sh", c][:, 0:1],
+                        op0=ALU.mult,
+                        op1=ALU.add,
+                    )
+            elif k == "oT":
+                c, h = tok[1], tok[2]
+                ot = ps.tile([P, 4, P], F32, tag="tr", name="ot_%d_%d" % (c, h))
+                T["ot", c, h] = ot
+                for cc in range(4):
+                    col = P * (4 * h + cc)
+                    nc.tensor.transpose(ot[:, cc, :], T["y", c][:, col : col + P], ident[:])
+            elif k == "ev":
+                c, h = tok[1], tok[2]
+                o_sb = keep.tile([P, 4, P], F32, name="o_%d_%d" % (c, h))
+                if EVAC[c][h] == "S":
+                    nc.scalar.copy(out=o_sb[:], in_=T["ot", c, h][:])
+                else:
+                    nc.vector.tensor_copy(out=o_sb[:], in_=T["ot", c, h][:])
+                nc.sync.dma_start(out=out_view[:, 4 * h : 4 * h + 4, P * c : P * (c + 1)], in_=o_sb[:])
+            else:
+                assert False, k
+
+        for tok in SCHED:
+            step(tok)

@@ -20,29 +20,29 @@ SLOPE = 0.01
 FLOPS = 2 * NQ * K * F * 2
 
 STAT = ["V","V","V","V"]
-NORM = [["G","G"],["G","G"],["G","G"],["V","G"]]
-EVAC = [["S","S"],["S","S"],["S","S"],["S","V"]]
+NORM = [["S","G"],["G","G"],["G","G"],["V","G"]]
+EVAC = [["S","S"],["S","S"],["S","S"],["S","S"]]
 SCHED = (
-    ("vf1",), ("vT1",), ("rg", "w1a", "V"), ("xT", 0), ("vc1",), ("qw", "w1a"),
-    ("rg", "w1b", "V"), ("xc", 0, "S"), ("xT", 1), ("qw", "w1b"), ("xq", 0), ("xT", 2),
-    ("xc", 1, "S"), ("m1", 0), ("xc", 2, "S"), ("xq", 1), ("xT", 3), ("s1", 0, 0),
-    ("xq", 2), ("m1", 1), ("s1", 0, 1), ("rg", "w2", "V"), ("s1", 0, 2), ("m1", 2),
-    ("s1", 0, 3), ("s1", 1, 0), ("lk", 0), ("s1", 1, 1), ("s1", 1, 2), ("s1", 1, 3),
-    ("xc", 3, "S"), ("hq", 0), ("lk", 1), ("vf2",), ("s1", 2, 0), ("vT2",),
-    ("s1", 2, 1), ("vc2",), ("hq", 1), ("s1", 2, 2), ("xq", 3), ("s1", 2, 3),
-    ("qw", "w2"), ("m1", 3), ("lk", 2), ("s1", 3, 0), ("m2", 0, 0), ("s1", 3, 1),
-    ("m2", 1, 0), ("s1", 3, 2), ("s1", 3, 3), ("hq", 2), ("a0", 0, 0), ("lk", 3),
-    ("a0", 1, 0), ("hq", 3), ("st", 0, 0), ("m2", 0, 1), ("m2", 1, 1), ("bn", 0, 0),
-    ("a0", 0, 1), ("m2", 2, 0), ("st", 1, 0), ("a0", 1, 1), ("a0", 2, 0), ("st", 0, 1),
-    ("m2", 3, 0), ("bn", 0, 1), ("a0", 3, 0), ("m2", 2, 1), ("ag", 0), ("a0", 2, 1),
-    ("bn", 1, 0), ("rs", 0), ("st", 1, 1), ("ab", 0), ("m2", 3, 1), ("bn", 1, 1),
-    ("nm", 0, 0), ("a0", 3, 1), ("ag", 1), ("st", 2, 0), ("nm", 0, 1), ("oT", 0, 0),
-    ("rs", 1), ("bn", 2, 0), ("ev", 0, 0), ("oT", 0, 1), ("ab", 1), ("st", 2, 1),
-    ("ev", 0, 1), ("nm", 1, 0), ("bn", 2, 1), ("nm", 1, 1), ("oT", 1, 0), ("ag", 2),
-    ("st", 3, 0), ("rs", 2), ("oT", 1, 1), ("ev", 1, 0), ("ab", 2), ("bn", 3, 0),
-    ("ev", 1, 1), ("nm", 2, 0), ("st", 3, 1), ("nm", 2, 1), ("oT", 2, 0), ("bn", 3, 1),
-    ("ev", 2, 0), ("oT", 2, 1), ("ag", 3), ("rs", 3), ("ev", 2, 1), ("ab", 3),
-    ("nm", 3, 0), ("nm", 3, 1), ("oT", 3, 0), ("oT", 3, 1), ("ev", 3, 0), ("ev", 3, 1),
+    ("vf1",), ("rg", "w1a", "V"), ("xT", 0), ("rg", "w1b", "V"), ("vT1",), ("xT", 1),
+    ("qw", "w1a"), ("xc", 0, "S"), ("qw", "w1b"), ("vc1",), ("xT", 2), ("xq", 0),
+    ("xc", 1, "V"), ("m1", 0), ("xc", 2, "S"), ("xq", 1), ("rg", "w2", "V"), ("s1", 0, 0),
+    ("xT", 3), ("s1", 0, 1), ("s1", 0, 2), ("m1", 1), ("s1", 0, 3), ("xq", 2),
+    ("xc", 3, "S"), ("qw", "w2"), ("s1", 1, 1), ("m1", 2), ("lk", 0), ("s1", 1, 0),
+    ("s1", 1, 2), ("s1", 1, 3), ("xq", 3), ("s1", 2, 1), ("lk", 1), ("s1", 2, 3),
+    ("m1", 3), ("s1", 2, 2), ("s1", 2, 0), ("s1", 3, 1), ("hq", 0), ("hq", 1),
+    ("s1", 3, 3), ("lk", 2), ("s1", 3, 2), ("m2", 0, 0), ("s1", 3, 0), ("m2", 1, 0),
+    ("vf2",), ("a0", 0, 0), ("lk", 3), ("vT2",), ("m2", 2, 0), ("a0", 1, 0),
+    ("vc2",), ("hq", 2), ("hq", 3), ("st", 1, 0), ("m2", 0, 1), ("st", 0, 0),
+    ("m2", 1, 1), ("a0", 0, 1), ("bn", 1, 0), ("m2", 3, 1), ("a0", 1, 1), ("m2", 2, 1),
+    ("bn", 0, 0), ("a0", 2, 0), ("st", 0, 1), ("a0", 2, 1), ("st", 1, 1), ("m2", 3, 0),
+    ("a0", 3, 1), ("bn", 0, 1), ("bn", 1, 1), ("ag", 0), ("st", 2, 0), ("rs", 0),
+    ("ag", 1), ("st", 2, 1), ("rs", 1), ("a0", 3, 0), ("ab", 0), ("bn", 2, 0),
+    ("nm", 0, 1), ("nm", 0, 0), ("bn", 2, 1), ("oT", 0, 1), ("ab", 1), ("ag", 2),
+    ("st", 3, 0), ("nm", 1, 0), ("oT", 0, 0), ("rs", 2), ("ev", 0, 1), ("st", 3, 1),
+    ("nm", 1, 1), ("oT", 1, 0), ("ev", 0, 0), ("ab", 2), ("bn", 3, 0), ("nm", 2, 1),
+    ("oT", 1, 1), ("ev", 1, 0), ("bn", 3, 1), ("nm", 2, 0), ("oT", 2, 1), ("ev", 1, 1),
+    ("ag", 3), ("rs", 3), ("oT", 2, 0), ("ev", 2, 1), ("ab", 3), ("nm", 3, 0),
+    ("nm", 3, 1), ("ev", 2, 0), ("oT", 3, 0), ("oT", 3, 1), ("ev", 3, 0), ("ev", 3, 1),
 )
 
 
@@ -227,7 +227,7 @@ def tile_attention_prop_pa_kernel(tc, x, w1, b1, w2, b2, gamma, beta, out):
                 nc.scalar.mul(out=T["a0", c, h][:], in_=T["l2", c, h][:], mul=SLOPE)
             elif k == "st":
                 c, h = tok[1], tok[2]
-                if h == 0:
+                if ("q", c) not in T:
                     T["q", c] = keep.tile([P, NQ], F32, name="q%d" % c)
                     T["stats", c] = keep.tile([P, 2, 6], F32, name="stats%d" % c)
                 nc.vector.scalar_tensor_tensor(
@@ -268,7 +268,7 @@ def tile_attention_prop_pa_kernel(tc, x, w1, b1, w2, b2, gamma, beta, out):
                 )
             elif k == "nm":
                 c, h = tok[1], tok[2]
-                if h == 0:
+                if ("y", c) not in T:
                     T["y", c] = keep.tile([P, NQ], F32, name="y%d" % c)
                 cols = slice(512 * h, 512 * (h + 1))
                 eng = NORM[c][h]

@@ -19,30 +19,31 @@ EPS = 1e-5
 SLOPE = 0.01
 FLOPS = 2 * NQ * K * F * 2
 
-STAT = ["V","V","V","V"]
-NORM = [["S","G"],["G","G"],["G","G"],["V","G"]]
+STAT = ["V","S","V","V"]
+NORM = [["G","G"],["S","G"],["V","G"],["V","G"]]
+LEAK = ["V","V","G","V"]
 EVAC = [["S","S"],["S","S"],["S","S"],["S","S"]]
 SCHED = (
-    ("vf1",), ("rg", "w1a", "V"), ("xT", 0), ("rg", "w1b", "V"), ("vT1",), ("xT", 1),
-    ("qw", "w1a"), ("xc", 0, "S"), ("qw", "w1b"), ("vc1",), ("xT", 2), ("xq", 0),
-    ("xc", 1, "V"), ("m1", 0), ("xc", 2, "S"), ("xq", 1), ("rg", "w2", "V"), ("s1", 0, 0),
-    ("xT", 3), ("s1", 0, 1), ("s1", 0, 2), ("m1", 1), ("s1", 0, 3), ("xq", 2),
-    ("xc", 3, "S"), ("qw", "w2"), ("s1", 1, 1), ("m1", 2), ("lk", 0), ("s1", 1, 0),
-    ("s1", 1, 2), ("s1", 1, 3), ("xq", 3), ("s1", 2, 1), ("lk", 1), ("s1", 2, 3),
-    ("m1", 3), ("s1", 2, 2), ("s1", 2, 0), ("s1", 3, 1), ("hq", 0), ("hq", 1),
-    ("s1", 3, 3), ("lk", 2), ("s1", 3, 2), ("m2", 0, 0), ("s1", 3, 0), ("m2", 1, 0),
-    ("vf2",), ("a0", 0, 0), ("lk", 3), ("vT2",), ("m2", 2, 0), ("a0", 1, 0),
-    ("vc2",), ("hq", 2), ("hq", 3), ("st", 1, 0), ("m2", 0, 1), ("st", 0, 0),
-    ("m2", 1, 1), ("a0", 0, 1), ("bn", 1, 0), ("m2", 3, 1), ("a0", 1, 1), ("m2", 2, 1),
-    ("bn", 0, 0), ("a0", 2, 0), ("st", 0, 1), ("a0", 2, 1), ("st", 1, 1), ("m2", 3, 0),
-    ("a0", 3, 1), ("bn", 0, 1), ("bn", 1, 1), ("ag", 0), ("st", 2, 0), ("rs", 0),
-    ("ag", 1), ("st", 2, 1), ("rs", 1), ("a0", 3, 0), ("ab", 0), ("bn", 2, 0),
-    ("nm", 0, 1), ("nm", 0, 0), ("bn", 2, 1), ("oT", 0, 1), ("ab", 1), ("ag", 2),
-    ("st", 3, 0), ("nm", 1, 0), ("oT", 0, 0), ("rs", 2), ("ev", 0, 1), ("st", 3, 1),
-    ("nm", 1, 1), ("oT", 1, 0), ("ev", 0, 0), ("ab", 2), ("bn", 3, 0), ("nm", 2, 1),
-    ("oT", 1, 1), ("ev", 1, 0), ("bn", 3, 1), ("nm", 2, 0), ("oT", 2, 1), ("ev", 1, 1),
-    ("ag", 3), ("rs", 3), ("oT", 2, 0), ("ev", 2, 1), ("ab", 3), ("nm", 3, 0),
-    ("nm", 3, 1), ("ev", 2, 0), ("oT", 3, 0), ("oT", 3, 1), ("ev", 3, 0), ("ev", 3, 1),
+    ("vf1",), ("vT1",), ("rg", "w1a", "V"), ("xT", 0), ("vc1",), ("qw", "w1a"),
+    ("rg", "w1b", "V"), ("xT", 1), ("xc", 0, "S"), ("xT", 2), ("xq", 0), ("xc", 1, "S"),
+    ("qw", "w1b"), ("m1", 0), ("xq", 1), ("xc", 2, "S"), ("rg", "w2", "V"), ("s1", 0, 1),
+    ("xT", 3), ("s1", 0, 0), ("s1", 0, 3), ("m1", 1), ("xq", 2), ("s1", 0, 2),
+    ("qw", "w2"), ("xc", 3, "S"), ("lk", 0), ("s1", 1, 0), ("m1", 2), ("s1", 1, 1),
+    ("s1", 1, 3), ("s1", 1, 2), ("xq", 3), ("s1", 2, 0), ("lk", 1), ("m1", 3),
+    ("s1", 2, 3), ("vf2",), ("s1", 2, 1), ("s1", 2, 2), ("vT2",), ("hq", 0),
+    ("s1", 3, 1), ("hq", 1), ("s1", 3, 3), ("lk", 2), ("s1", 3, 0), ("m2", 1, 0),
+    ("s1", 3, 2), ("m2", 0, 0), ("vc2",), ("lk", 3), ("a0", 1, 0), ("m2", 2, 0),
+    ("m2", 3, 0), ("a0", 0, 0), ("hq", 2), ("a0", 2, 0), ("hq", 3), ("st", 0, 0),
+    ("a0", 3, 0), ("m2", 0, 1), ("st", 2, 0), ("st", 1, 0), ("m2", 1, 1), ("a0", 0, 1),
+    ("m2", 2, 1), ("bn", 0, 0), ("a0", 1, 1), ("m2", 3, 1), ("st", 0, 1), ("a0", 2, 1),
+    ("st", 1, 1), ("bn", 1, 0), ("st", 2, 1), ("bn", 0, 1), ("bn", 1, 1), ("ag", 0),
+    ("bn", 2, 0), ("rs", 0), ("ag", 1), ("ab", 0), ("st", 3, 0), ("rs", 1),
+    ("a0", 3, 1), ("nm", 0, 1), ("ab", 1), ("bn", 2, 1), ("nm", 0, 0), ("nm", 1, 0),
+    ("oT", 0, 1), ("nm", 1, 1), ("ag", 2), ("bn", 3, 0), ("oT", 0, 0), ("rs", 2),
+    ("ev", 0, 1), ("st", 3, 1), ("oT", 1, 0), ("ev", 0, 0), ("oT", 1, 1), ("ab", 2),
+    ("bn", 3, 1), ("ev", 1, 0), ("nm", 2, 1), ("ag", 3), ("nm", 2, 0), ("oT", 2, 1),
+    ("rs", 3), ("ev", 1, 1), ("ab", 3), ("oT", 2, 0), ("nm", 3, 0), ("nm", 3, 1),
+    ("ev", 2, 1), ("oT", 3, 0), ("ev", 2, 0), ("oT", 3, 1), ("ev", 3, 0), ("ev", 3, 1),
 )
 
 
@@ -103,6 +104,7 @@ def tile_attention_prop_pa_kernel(tc, x, w1, b1, w2, b2, gamma, beta, out):
         rT = keep.tile([P, 12], F32, name="rT")
         b2s = keep.tile([P, 4], F32, name="b2s")
         gpair = keep.tile([P, 4, 2], F32, name="gpair")
+        negc = keep.tile([P, 4], F32, name="negc")
         out_view = out.rearrange("(i c) f -> i c f", c=8)
 
         def step(tok):
@@ -126,6 +128,9 @@ def tile_attention_prop_pa_kernel(tc, x, w1, b1, w2, b2, gamma, beta, out):
                 nc.scalar.mul(out=b2s[:], in_=rT[:, 0:4], mul=1.0 - SLOPE)
                 nc.scalar.copy(out=gpair[:, :, 0], in_=rT[:, 4:8])
                 nc.scalar.mul(out=gpair[:, :, 1], in_=rT[:, 4:8], mul=-1.0)
+                T["posc"] = keep.tile([P, 4], F32, name="posc")
+                nc.scalar.activation(out=T["posc"][:], in_=b2s[:], func=ACT.Relu)
+                nc.scalar.mul(out=negc[:], in_=T["posc"][:], mul=-1.0)
             elif k == "rg":
                 nm = tok[1]
                 width = wdst[nm][3]
@@ -224,32 +229,96 @@ def tile_attention_prop_pa_kernel(tc, x, w1, b1, w2, b2, gamma, beta, out):
             elif k == "a0":
                 c, h = tok[1], tok[2]
                 T["a0", c, h] = keep.tile([P, 512], F32, name="a0_%d_%d" % (c, h))
-                nc.scalar.mul(out=T["a0", c, h][:], in_=T["l2", c, h][:], mul=SLOPE)
+                if LEAK[c] == "G":
+                    nc.scalar.activation(
+                        out=T["a0", c, h][:], in_=T["l2", c, h][:], func=ACT.Identity, bias=rT[:, c : c + 1], scale=1.0
+                    )
+                else:
+                    nc.scalar.mul(out=T["a0", c, h][:], in_=T["l2", c, h][:], mul=SLOPE)
             elif k == "st":
                 c, h = tok[1], tok[2]
                 if ("q", c) not in T:
                     T["q", c] = keep.tile([P, NQ], F32, name="q%d" % c)
-                    T["stats", c] = keep.tile([P, 2, 6], F32, name="stats%d" % c)
-                nc.vector.scalar_tensor_tensor(
-                    out=T["q", c][:, 512 * h : 512 * (h + 1)],
-                    in0=T["l2", c, h][:],
-                    scalar=b2s[:, c : c + 1],
-                    in1=T["a0", c, h][:],
-                    op0=ALU.add,
-                    op1=ALU.max,
-                )
+                    if STAT[c] == "S":
+                        T["ssum", c] = keep.tile([P, 2], F32, name="ssum%d" % c)
+                        T["ssq", c] = keep.tile([P, 2], F32, name="ssq%d" % c)
+                    else:
+                        T["stats", c] = keep.tile([P, 2, 6], F32, name="stats%d" % c)
+                if LEAK[c] == "G":
+                    neg = keep.tile([P, 512], F32, name="neg_%d_%d" % (c, h))
+                    nc.gpsimd.tensor_scalar(
+                        out=neg[:], in0=T["a0", c, h][:], scalar1=SLOPE - 1.0, scalar2=0.0, op0=ALU.mult, op1=ALU.max
+                    )
+                    nc.gpsimd.tensor_tensor(
+                        out=T["q", c][:, 512 * h : 512 * (h + 1)], in0=T["a0", c, h][:], in1=neg[:], op=ALU.add
+                    )
+                else:
+                    nc.vector.scalar_tensor_tensor(
+                        out=T["q", c][:, 512 * h : 512 * (h + 1)],
+                        in0=T["l2", c, h][:],
+                        scalar=b2s[:, c : c + 1],
+                        in1=T["a0", c, h][:],
+                        op0=ALU.add,
+                        op1=ALU.max,
+                        accum_out=T["ssum", c][:, h : h + 1] if STAT[c] == "S" else None,
+                    )
             elif k == "bn":
                 c, h = tok[1], tok[2]
-                nc.vector.bn_stats(out=T["stats", c][:, h, :], in_=T["q", c][:, 512 * h : 512 * (h + 1)])
+                if STAT[c] == "S":
+                    junk = keep.tile([P, 512], BF16, name="junk_%d_%d" % (c, h))
+                    nc.scalar.activation(
+                        out=junk[:],
+                        in_=T["q", c][:, 512 * h : 512 * (h + 1)],
+                        func=ACT.Square,
+                        bias=negc[:, c : c + 1],
+                        scale=1.0,
+                        accum_out=T["ssq", c][:, h : h + 1],
+                    )
+                else:
+                    nc.vector.bn_stats(out=T["stats", c][:, h, :], in_=T["q", c][:, 512 * h : 512 * (h + 1)])
             elif k == "ag":
                 c = tok[1]
                 T["mv", c] = keep.tile([P, 2], F32, name="mv%d" % c)
-                nc.vector.bn_aggr(out=T["mv", c][:], in_=T["stats", c][:].rearrange("p a b -> p (a b)"))
+                if STAT[c] == "S":
+                    ms = keep.tile([P, 2], F32, name="ms%d" % c)
+                    nc.vector.tensor_scalar(
+                        out=T["mv", c][:, 0:1],
+                        in0=T["ssum", c][:, 0:1],
+                        scalar1=T["ssum", c][:, 1:2],
+                        scalar2=1.0 / NQ,
+                        op0=ALU.add,
+                        op1=ALU.mult,
+                    )
+                    nc.vector.tensor_scalar(
+                        out=ms[:, 0:1],
+                        in0=T["ssq", c][:, 0:1],
+                        scalar1=T["ssq", c][:, 1:2],
+                        scalar2=1.0 / NQ,
+                        op0=ALU.add,
+                        op1=ALU.mult,
+                    )
+                    nc.vector.tensor_scalar(
+                        out=ms[:, 1:2], in0=T["mv", c][:, 0:1], scalar1=negc[:, c : c + 1], scalar2=None, op0=ALU.add
+                    )
+                    nc.vector.scalar_tensor_tensor(
+                        out=T["mv", c][:, 1:2],
+                        in0=ms[:, 1:2],
+                        scalar=ms[:, 1:2],
+                        in1=ms[:, 0:1],
+                        op0=ALU.mult,
+                        op1=ALU.subtract,
+                    )
+                else:
+                    nc.vector.bn_aggr(out=T["mv", c][:], in_=T["stats", c][:].rearrange("p a b -> p (a b)"))
             elif k == "rs":
                 c = tok[1]
                 T["rstd", c] = keep.tile([P, 1], F32, name="rstd%d" % c)
                 nc.scalar.activation(
-                    out=T["rstd", c][:], in_=T["mv", c][:, 1:2], func=ACT.Abs_reciprocal_sqrt, bias=EPS, scale=1.0
+                    out=T["rstd", c][:],
+                    in_=T["mv", c][:, 1:2],
+                    func=ACT.Abs_reciprocal_sqrt,
+                    bias=EPS,
+                    scale=-1.0 if STAT[c] == "S" else 1.0,
                 )
             elif k == "ab":
                 c = tok[1]

@@ -20,30 +20,31 @@ SLOPE = 0.01
 FLOPS = 2 * NQ * K * F * 2
 
 STAT = ["V","S","V","V"]
-NORM = [["G","G"],["S","G"],["V","G"],["V","G"]]
-LEAK = ["V","V","G","V"]
-EVAC = [["S","S"],["S","S"],["S","S"],["S","S"]]
+NORM = [["S","S"],["G","G"],["G","S"],["V","V"]]
+LEAK = ["V","V","V","V"]
+ABENG = ["G","G","G","G"]
+EVAC = [["S","S"],["V","V"],["V","S"],["S","S"]]
 SCHED = (
-    ("vf1",), ("vT1",), ("rg", "w1a", "V"), ("xT", 0), ("vc1",), ("qw", "w1a"),
-    ("rg", "w1b", "V"), ("xT", 1), ("xc", 0, "S"), ("xT", 2), ("xq", 0), ("xc", 1, "S"),
-    ("qw", "w1b"), ("m1", 0), ("xq", 1), ("xc", 2, "S"), ("rg", "w2", "V"), ("s1", 0, 1),
-    ("xT", 3), ("s1", 0, 0), ("s1", 0, 3), ("m1", 1), ("xq", 2), ("s1", 0, 2),
-    ("qw", "w2"), ("xc", 3, "S"), ("lk", 0), ("s1", 1, 0), ("m1", 2), ("s1", 1, 1),
-    ("s1", 1, 3), ("s1", 1, 2), ("xq", 3), ("s1", 2, 0), ("lk", 1), ("m1", 3),
-    ("s1", 2, 3), ("vf2",), ("s1", 2, 1), ("s1", 2, 2), ("vT2",), ("hq", 0),
-    ("s1", 3, 1), ("hq", 1), ("s1", 3, 3), ("lk", 2), ("s1", 3, 0), ("m2", 1, 0),
-    ("s1", 3, 2), ("m2", 0, 0), ("vc2",), ("lk", 3), ("a0", 1, 0), ("m2", 2, 0),
-    ("m2", 3, 0), ("a0", 0, 0), ("hq", 2), ("a0", 2, 0), ("hq", 3), ("st", 0, 0),
-    ("a0", 3, 0), ("m2", 0, 1), ("st", 2, 0), ("st", 1, 0), ("m2", 1, 1), ("a0", 0, 1),
-    ("m2", 2, 1), ("bn", 0, 0), ("a0", 1, 1), ("m2", 3, 1), ("st", 0, 1), ("a0", 2, 1),
-    ("st", 1, 1), ("bn", 1, 0), ("st", 2, 1), ("bn", 0, 1), ("bn", 1, 1), ("ag", 0),
-    ("bn", 2, 0), ("rs", 0), ("ag", 1), ("ab", 0), ("st", 3, 0), ("rs", 1),
-    ("a0", 3, 1), ("nm", 0, 1), ("ab", 1), ("bn", 2, 1), ("nm", 0, 0), ("nm", 1, 0),
-    ("oT", 0, 1), ("nm", 1, 1), ("ag", 2), ("bn", 3, 0), ("oT", 0, 0), ("rs", 2),
-    ("ev", 0, 1), ("st", 3, 1), ("oT", 1, 0), ("ev", 0, 0), ("oT", 1, 1), ("ab", 2),
-    ("bn", 3, 1), ("ev", 1, 0), ("nm", 2, 1), ("ag", 3), ("nm", 2, 0), ("oT", 2, 1),
-    ("rs", 3), ("ev", 1, 1), ("ab", 3), ("oT", 2, 0), ("nm", 3, 0), ("nm", 3, 1),
-    ("ev", 2, 1), ("oT", 3, 0), ("ev", 2, 0), ("oT", 3, 1), ("ev", 3, 0), ("ev", 3, 1),
+    ("rg", "w1a", "V"), ("xT", 0), ("rg", "w1b", "V"), ("xc", 0, "S"), ("vf1",), ("qw", "w1b"),
+    ("xT", 1), ("qw", "w1a"), ("xq", 0), ("xT", 2), ("xc", 1, "V"), ("vT1",),
+    ("m1", 0), ("xc", 2, "S"), ("vc1",), ("xq", 1), ("s1", 0, 0), ("xT", 3),
+    ("xq", 2), ("s1", 0, 1), ("rg", "w2", "V"), ("s1", 0, 2), ("m1", 1), ("s1", 0, 3),
+    ("xc", 3, "S"), ("lk", 0), ("m1", 2), ("s1", 1, 0), ("s1", 1, 1), ("s1", 1, 2),
+    ("qw", "w2"), ("s1", 1, 3), ("s1", 2, 1), ("xq", 3), ("s1", 2, 3), ("lk", 1),
+    ("s1", 2, 2), ("m1", 3), ("s1", 2, 0), ("vf2",), ("s1", 3, 0), ("hq", 0),
+    ("vT2",), ("hq", 1), ("s1", 3, 2), ("lk", 2), ("s1", 3, 3), ("m2", 0, 0),
+    ("s1", 3, 1), ("m2", 2, 0), ("vc2",), ("lk", 3), ("m2", 1, 0), ("a0", 0, 0),
+    ("m2", 3, 0), ("a0", 2, 0), ("hq", 2), ("a0", 1, 0), ("hq", 3), ("st", 0, 0),
+    ("a0", 3, 0), ("m2", 0, 1), ("st", 1, 0), ("m2", 1, 1), ("a0", 0, 1), ("m2", 2, 1),
+    ("bn", 0, 0), ("a0", 1, 1), ("m2", 3, 1), ("st", 0, 1), ("a0", 2, 1), ("st", 1, 1),
+    ("bn", 1, 0), ("bn", 0, 1), ("bn", 1, 1), ("st", 2, 0), ("a0", 3, 1), ("ag", 1),
+    ("ag", 0), ("st", 2, 1), ("rs", 0), ("bn", 2, 0), ("ab", 0), ("rs", 1),
+    ("bn", 2, 1), ("ab", 1), ("nm", 0, 1), ("st", 3, 0), ("nm", 1, 0), ("nm", 0, 0),
+    ("oT", 0, 1), ("ag", 2), ("st", 3, 1), ("oT", 0, 0), ("nm", 1, 1), ("rs", 2),
+    ("ev", 0, 1), ("bn", 3, 0), ("oT", 1, 0), ("ab", 2), ("ev", 0, 0), ("bn", 3, 1),
+    ("oT", 1, 1), ("nm", 2, 0), ("nm", 2, 1), ("ag", 3), ("ev", 1, 0), ("rs", 3),
+    ("oT", 2, 1), ("ev", 1, 1), ("ab", 3), ("oT", 2, 0), ("nm", 3, 0), ("ev", 2, 1),
+    ("nm", 3, 1), ("oT", 3, 0), ("ev", 2, 0), ("oT", 3, 1), ("ev", 3, 0), ("ev", 3, 1),
 )
 
 
@@ -51,7 +52,14 @@ def tile_attention_prop_pa_kernel(tc, x, w1, b1, w2, b2, gamma, beta, out):
     nc = tc.nc
     with ExitStack() as ctx:
         keep = ctx.enter_context(tc.tile_pool(name="keep", bufs=1))
-        ps = ctx.enter_context(tc.psum_pool(name="ps", bufs=4))
+        ps = ctx.enter_context(tc.psum_pool(name="ps", bufs=1))
+        used = [0]
+
+        def new_bank(shape, name):
+            slot = used[0] % 8
+            used[0] = used[0] + 1
+            return ps.tile(shape, F32, tag="bank%d" % slot, name=name)
+
         ctx.enter_context(tc.manual_schedule())
         T = {}
 
@@ -113,7 +121,7 @@ def tile_attention_prop_pa_kernel(tc, x, w1, b1, w2, b2, gamma, beta, out):
                 T["vf1"] = keep.tile([P, P], F32, name="vf1")
                 nc.vector.tensor_copy(out=T["vf1"][:], in_=vb1[:])
             elif k == "vT1":
-                T["vp1"] = ps.tile([P, P], F32, tag="tr", name="vp1")
+                T["vp1"] = new_bank([P, P], "vp1")
                 nc.tensor.transpose(T["vp1"][:], T["vf1"][:], ident[:])
             elif k == "vc1":
                 nc.vector.tensor_copy(out=b1T[:], in_=T["vp1"][:, 0:4])
@@ -121,7 +129,7 @@ def tile_attention_prop_pa_kernel(tc, x, w1, b1, w2, b2, gamma, beta, out):
                 T["vf2"] = keep.tile([P, P], F32, name="vf2")
                 nc.scalar.copy(out=T["vf2"][:], in_=vr[:])
             elif k == "vT2":
-                T["vp2"] = ps.tile([P, P], F32, tag="tr", name="vp2")
+                T["vp2"] = new_bank([P, P], "vp2")
                 nc.tensor.transpose(T["vp2"][:], T["vf2"][:], ident[:])
             elif k == "vc2":
                 nc.scalar.copy(out=rT[:], in_=T["vp2"][:, 0:12])
@@ -152,7 +160,7 @@ def tile_attention_prop_pa_kernel(tc, x, w1, b1, w2, b2, gamma, beta, out):
                 )
             elif k == "xT":
                 j = tok[1]
-                xt = ps.tile([P, 2, 2, P], F32, tag="tr", name="xt%d" % j)
+                xt = new_bank([P, 2, 2, P], "xt%d" % j)
                 T["xt", j] = xt
                 xw = x_sb[j][:].bitcast(F32).rearrange("i (cc w u) -> i cc u w", cc=2, u=2)
                 for cc in range(2):
@@ -177,7 +185,7 @@ def tile_attention_prop_pa_kernel(tc, x, w1, b1, w2, b2, gamma, beta, out):
                 sl = slice(256 * pi, 256 * (pi + 1))
                 T["v", pi] = keep.tile([P, 4, 256], F32, name="v%d" % pi)
                 for tp in range(2):
-                    bank = ps.tile([P, 2, 256], F32, tag="mm", name="l1_%d_%d" % (pi, tp))
+                    bank = new_bank([P, 2, 256], "l1_%d_%d" % (pi, tp))
                     T["l1", pi, tp] = bank
                     for e in range(2):
                         t = 2 * tp + e
@@ -215,7 +223,7 @@ def tile_attention_prop_pa_kernel(tc, x, w1, b1, w2, b2, gamma, beta, out):
                 c, h = tok[1], tok[2]
                 fs = slice(P * c, P * (c + 1))
                 cols = slice(512 * h, 512 * (h + 1))
-                p2 = ps.tile([P, 512], F32, tag="mm", name="l2_%d_%d" % (c, h))
+                p2 = new_bank([P, 512], "l2_%d_%d" % (c, h))
                 T["l2", c, h] = p2
                 nc.tensor.matmul_mx(
                     out=p2[:],
@@ -281,7 +289,7 @@ def tile_attention_prop_pa_kernel(tc, x, w1, b1, w2, b2, gamma, beta, out):
                 T["mv", c] = keep.tile([P, 2], F32, name="mv%d" % c)
                 if STAT[c] == "S":
                     ms = keep.tile([P, 2], F32, name="ms%d" % c)
-                    nc.vector.tensor_scalar(
+                    nc.gpsimd.tensor_scalar(
                         out=T["mv", c][:, 0:1],
                         in0=T["ssum", c][:, 0:1],
                         scalar1=T["ssum", c][:, 1:2],
@@ -289,7 +297,7 @@ def tile_attention_prop_pa_kernel(tc, x, w1, b1, w2, b2, gamma, beta, out):
                         op0=ALU.add,
                         op1=ALU.mult,
                     )
-                    nc.vector.tensor_scalar(
+                    nc.gpsimd.tensor_scalar(
                         out=ms[:, 0:1],
                         in0=T["ssq", c][:, 0:1],
                         scalar1=T["ssq", c][:, 1:2],
@@ -297,14 +305,14 @@ def tile_attention_prop_pa_kernel(tc, x, w1, b1, w2, b2, gamma, beta, out):
                         op0=ALU.add,
                         op1=ALU.mult,
                     )
-                    nc.vector.tensor_scalar(
-                        out=ms[:, 1:2], in0=T["mv", c][:, 0:1], scalar1=negc[:, c : c + 1], scalar2=None, op0=ALU.add
+                    nc.gpsimd.tensor_scalar(
+                        out=ms[:, 1:2], in0=T["mv", c][:, 0:1], scalar1=negc[:, c : c + 1], scalar2=0.0, op0=ALU.add, op1=ALU.add
                     )
-                    nc.vector.scalar_tensor_tensor(
+                    nc.gpsimd.tensor_scalar(
                         out=T["mv", c][:, 1:2],
                         in0=ms[:, 1:2],
-                        scalar=ms[:, 1:2],
-                        in1=ms[:, 0:1],
+                        scalar1=ms[:, 1:2],
+                        scalar2=ms[:, 0:1],
                         op0=ALU.mult,
                         op1=ALU.subtract,
                     )
@@ -324,14 +332,15 @@ def tile_attention_prop_pa_kernel(tc, x, w1, b1, w2, b2, gamma, beta, out):
                 c = tok[1]
                 T["ab", c] = keep.tile([P, 2], F32, name="ab%d" % c)
                 T["sh", c] = keep.tile([P, 1], F32, name="sh%d" % c)
-                nc.vector.tensor_scalar(
-                    out=T["ab", c][:], in0=gpair[:, c, :], scalar1=T["rstd", c][:, 0:1], scalar2=None, op0=ALU.mult
+                e = nc.gpsimd if ABENG[c] == "G" else nc.vector
+                e.tensor_scalar(
+                    out=T["ab", c][:], in0=gpair[:, c, :], scalar1=T["rstd", c][:, 0:1], scalar2=0.0, op0=ALU.mult, op1=ALU.add
                 )
-                nc.vector.scalar_tensor_tensor(
+                e.tensor_scalar(
                     out=T["sh", c][:],
                     in0=T["mv", c][:, 0:1],
-                    scalar=T["ab", c][:, 1:2],
-                    in1=rT[:, 8 + c : 9 + c],
+                    scalar1=T["ab", c][:, 1:2],
+                    scalar2=rT[:, 8 + c : 9 + c],
                     op0=ALU.mult,
                     op1=ALU.add,
                 )
@@ -361,7 +370,7 @@ def tile_attention_prop_pa_kernel(tc, x, w1, b1, w2, b2, gamma, beta, out):
                     )
             elif k == "oT":
                 c, h = tok[1], tok[2]
-                ot = ps.tile([P, 4, P], F32, tag="tr", name="ot_%d_%d" % (c, h))
+                ot = new_bank([P, 4, P], "ot_%d_%d" % (c, h))
                 T["ot", c, h] = ot
                 for cc in range(4):
                     col = P * (4 * h + cc)

@@ -20,31 +20,32 @@ SLOPE = 0.01
 FLOPS = 2 * NQ * K * F * 2
 
 STAT = ["V","S","V","V"]
-NORM = [["S","S"],["G","G"],["G","S"],["V","V"]]
+NORM = [["S","G"],["S","G"],["G","V"],["V","V"]]
 LEAK = ["V","V","V","V"]
-ABENG = ["G","G","G","G"]
-EVAC = [["S","S"],["V","V"],["V","S"],["S","S"]]
+ABENG = ["V","V","G","V"]
+EVAC = [["S","S"],["S","V"],["S","S"],["V","S"]]
 SCHED = (
-    ("rg", "w1a", "V"), ("xT", 0), ("rg", "w1b", "V"), ("xc", 0, "S"), ("vf1",), ("qw", "w1b"),
-    ("xT", 1), ("qw", "w1a"), ("xq", 0), ("xT", 2), ("xc", 1, "V"), ("vT1",),
-    ("m1", 0), ("xc", 2, "S"), ("vc1",), ("xq", 1), ("s1", 0, 0), ("xT", 3),
-    ("xq", 2), ("s1", 0, 1), ("rg", "w2", "V"), ("s1", 0, 2), ("m1", 1), ("s1", 0, 3),
-    ("xc", 3, "S"), ("lk", 0), ("m1", 2), ("s1", 1, 0), ("s1", 1, 1), ("s1", 1, 2),
-    ("qw", "w2"), ("s1", 1, 3), ("s1", 2, 1), ("xq", 3), ("s1", 2, 3), ("lk", 1),
-    ("s1", 2, 2), ("m1", 3), ("s1", 2, 0), ("vf2",), ("s1", 3, 0), ("hq", 0),
-    ("vT2",), ("hq", 1), ("s1", 3, 2), ("lk", 2), ("s1", 3, 3), ("m2", 0, 0),
-    ("s1", 3, 1), ("m2", 2, 0), ("vc2",), ("lk", 3), ("m2", 1, 0), ("a0", 0, 0),
-    ("m2", 3, 0), ("a0", 2, 0), ("hq", 2), ("a0", 1, 0), ("hq", 3), ("st", 0, 0),
-    ("a0", 3, 0), ("m2", 0, 1), ("st", 1, 0), ("m2", 1, 1), ("a0", 0, 1), ("m2", 2, 1),
-    ("bn", 0, 0), ("a0", 1, 1), ("m2", 3, 1), ("st", 0, 1), ("a0", 2, 1), ("st", 1, 1),
-    ("bn", 1, 0), ("bn", 0, 1), ("bn", 1, 1), ("st", 2, 0), ("a0", 3, 1), ("ag", 1),
-    ("ag", 0), ("st", 2, 1), ("rs", 0), ("bn", 2, 0), ("ab", 0), ("rs", 1),
-    ("bn", 2, 1), ("ab", 1), ("nm", 0, 1), ("st", 3, 0), ("nm", 1, 0), ("nm", 0, 0),
-    ("oT", 0, 1), ("ag", 2), ("st", 3, 1), ("oT", 0, 0), ("nm", 1, 1), ("rs", 2),
-    ("ev", 0, 1), ("bn", 3, 0), ("oT", 1, 0), ("ab", 2), ("ev", 0, 0), ("bn", 3, 1),
-    ("oT", 1, 1), ("nm", 2, 0), ("nm", 2, 1), ("ag", 3), ("ev", 1, 0), ("rs", 3),
-    ("oT", 2, 1), ("ev", 1, 1), ("ab", 3), ("oT", 2, 0), ("nm", 3, 0), ("ev", 2, 1),
-    ("nm", 3, 1), ("oT", 3, 0), ("ev", 2, 0), ("oT", 3, 1), ("ev", 3, 0), ("ev", 3, 1),
+    ("xT", 0), ("vf1",), ("vT1",), ("xc", 0, "S"), ("xT", 1), ("rg", "w1a", "V"),
+    ("xq", 0), ("xT", 2), ("qw", "w1a"), ("xc", 1, "S"), ("rg", "w1b", "V"), ("m1", 0, 0),
+    ("qw", "w1b"), ("xc", 2, "S"), ("vc1",), ("rg", "w2", "V"), ("m1", 0, 1), ("s1", 0, 1),
+    ("s1", 0, 0), ("xT", 3), ("s1", 0, 3), ("xq", 1), ("s1", 0, 2), ("qw", "w2"),
+    ("m1", 1, 0), ("xq", 2), ("xc", 3, "S"), ("lk", 0), ("m1", 1, 1), ("s1", 1, 0),
+    ("m1", 2, 1), ("s1", 1, 1), ("s1", 1, 2), ("hq", 0), ("m1", 2, 0), ("s1", 1, 3),
+    ("xq", 3), ("s1", 2, 3), ("lk", 1), ("m1", 3, 0), ("s1", 2, 0), ("s1", 2, 1),
+    ("m1", 3, 1), ("s1", 2, 2), ("s1", 3, 0), ("hq", 1), ("s1", 3, 1), ("lk", 2),
+    ("m2", 0, 0), ("s1", 3, 3), ("s1", 3, 2), ("m2", 1, 0), ("vf2",), ("lk", 3),
+    ("a0", 0, 0), ("vT2",), ("m2", 2, 0), ("vc2",), ("hq", 2), ("a0", 1, 0),
+    ("hq", 3), ("st", 0, 0), ("a0", 2, 0), ("m2", 0, 1), ("st", 1, 0), ("m2", 1, 1),
+    ("a0", 0, 1), ("bn", 0, 0), ("m2", 3, 1), ("a0", 1, 1), ("m2", 2, 1), ("st", 0, 1),
+    ("bn", 1, 0), ("m2", 3, 0), ("st", 1, 1), ("a0", 2, 1), ("bn", 0, 1), ("bn", 1, 1),
+    ("st", 2, 1), ("ag", 1), ("ag", 0), ("st", 2, 0), ("rs", 0), ("a0", 3, 1),
+    ("ab", 0), ("bn", 2, 1), ("nm", 0, 0), ("nm", 0, 1), ("bn", 2, 0), ("rs", 1),
+    ("a0", 3, 0), ("oT", 0, 0), ("ab", 1), ("ag", 2), ("st", 3, 1), ("nm", 1, 0),
+    ("nm", 1, 1), ("oT", 0, 1), ("st", 3, 0), ("rs", 2), ("ev", 0, 0), ("oT", 1, 0),
+    ("ab", 2), ("bn", 3, 1), ("ev", 0, 1), ("oT", 1, 1), ("bn", 3, 0), ("nm", 2, 0),
+    ("ev", 1, 0), ("nm", 2, 1), ("ag", 3), ("ev", 1, 1), ("oT", 2, 1), ("rs", 3),
+    ("ab", 3), ("oT", 2, 0), ("nm", 3, 1), ("ev", 2, 1), ("nm", 3, 0), ("oT", 3, 1),
+    ("ev", 2, 0), ("oT", 3, 0), ("ev", 3, 1), ("ev", 3, 0),
 )
 
 
@@ -90,14 +91,14 @@ def tile_attention_prop_pa_kernel(tc, x, w1, b1, w2, b2, gamma, beta, out):
             x_sb[j] = keep.tile([P, 1024], BF16, name="x_sb%d" % j)
             nc.sync.dma_start(out=x_sb[j][:], in_=x_view[:, 1024 * j : 1024 * (j + 1)])
 
-        load_w1("w1a", 0)
         load_x(0)
-        load_w1("w1b", 256)
         load_x(1)
+        load_w1("w1a", 0)
         load_x(2)
-        load_x(3)
+        load_w1("w1b", 256)
         wsb["w2"] = keep.tile([P, 4, F], BF16, name="sb_w2")
         nc.sync.dma_start(out=wsb["w2"][:], in_=w2.rearrange("(t p) f -> p t f", p=P))
+        load_x(3)
 
         w1q = keep.tile([P, F], U32, align_bytes=64, name="w1q")
         w1s = keep.tile([P, F], U8, align_bytes=64, name="w1s")
@@ -183,8 +184,9 @@ def tile_attention_prop_pa_kernel(tc, x, w1, b1, w2, b2, gamma, beta, out):
             elif k == "m1":
                 pi = tok[1]
                 sl = slice(256 * pi, 256 * (pi + 1))
-                T["v", pi] = keep.tile([P, 4, 256], F32, name="v%d" % pi)
-                for tp in range(2):
+                if ("v", pi) not in T:
+                    T["v", pi] = keep.tile([P, 4, 256], F32, name="v%d" % pi)
+                for tp in (tok[2],):
                     bank = new_bank([P, 2, 256], "l1_%d_%d" % (pi, tp))
                     T["l1", pi, tp] = bank
                     for e in range(2):

@@ -12,381 +12,500 @@ ALU = mybir.AluOpType
 ACT = mybir.ActivationFunctionType
 
 P = 128
-NQ = 1024
-K = 512
-F = 512
+ROWS = 1024
+WIDTH = 512
+PACK = 4
+GROUPS = ROWS // P
+PIECE = 256
+W1_PART = 256
+HALF = 512
+BANKS = 8
 EPS = 1e-5
 SLOPE = 0.01
-FLOPS = 2 * NQ * K * F * 2
 
-STAT = ["V","S","V","V"]
-NORM = [["S","G"],["S","G"],["G","V"],["V","V"]]
-LEAK = ["V","V","V","V"]
-ABENG = ["V","V","G","V"]
-EVAC = [["S","S"],["S","V"],["S","S"],["V","S"]]
-SCHED = (
-    ("xT", 0), ("vf1",), ("vT1",), ("xc", 0, "S"), ("xT", 1), ("rg", "w1a", "V"),
-    ("xq", 0), ("xT", 2), ("qw", "w1a"), ("xc", 1, "S"), ("rg", "w1b", "V"), ("m1", 0, 0),
-    ("qw", "w1b"), ("xc", 2, "S"), ("vc1",), ("rg", "w2", "V"), ("m1", 0, 1), ("s1", 0, 1),
-    ("s1", 0, 0), ("xT", 3), ("s1", 0, 3), ("xq", 1), ("s1", 0, 2), ("qw", "w2"),
-    ("m1", 1, 0), ("xq", 2), ("xc", 3, "S"), ("lk", 0), ("m1", 1, 1), ("s1", 1, 0),
-    ("m1", 2, 1), ("s1", 1, 1), ("s1", 1, 2), ("hq", 0), ("m1", 2, 0), ("s1", 1, 3),
-    ("xq", 3), ("s1", 2, 3), ("lk", 1), ("m1", 3, 0), ("s1", 2, 0), ("s1", 2, 1),
-    ("m1", 3, 1), ("s1", 2, 2), ("s1", 3, 0), ("hq", 1), ("s1", 3, 1), ("lk", 2),
-    ("m2", 0, 0), ("s1", 3, 3), ("s1", 3, 2), ("m2", 1, 0), ("vf2",), ("lk", 3),
-    ("a0", 0, 0), ("vT2",), ("m2", 2, 0), ("vc2",), ("hq", 2), ("a0", 1, 0),
-    ("hq", 3), ("st", 0, 0), ("a0", 2, 0), ("m2", 0, 1), ("st", 1, 0), ("m2", 1, 1),
-    ("a0", 0, 1), ("bn", 0, 0), ("m2", 3, 1), ("a0", 1, 1), ("m2", 2, 1), ("st", 0, 1),
-    ("bn", 1, 0), ("m2", 3, 0), ("st", 1, 1), ("a0", 2, 1), ("bn", 0, 1), ("bn", 1, 1),
-    ("st", 2, 1), ("ag", 1), ("ag", 0), ("st", 2, 0), ("rs", 0), ("a0", 3, 1),
-    ("ab", 0), ("bn", 2, 1), ("nm", 0, 0), ("nm", 0, 1), ("bn", 2, 0), ("rs", 1),
-    ("a0", 3, 0), ("oT", 0, 0), ("ab", 1), ("ag", 2), ("st", 3, 1), ("nm", 1, 0),
-    ("nm", 1, 1), ("oT", 0, 1), ("st", 3, 0), ("rs", 2), ("ev", 0, 0), ("oT", 1, 0),
-    ("ab", 2), ("bn", 3, 1), ("ev", 0, 1), ("oT", 1, 1), ("bn", 3, 0), ("nm", 2, 0),
-    ("ev", 1, 0), ("nm", 2, 1), ("ag", 3), ("ev", 1, 1), ("oT", 2, 1), ("rs", 3),
-    ("ab", 3), ("oT", 2, 0), ("nm", 3, 1), ("ev", 2, 1), ("nm", 3, 0), ("oT", 3, 1),
-    ("ev", 2, 0), ("oT", 3, 0), ("ev", 3, 1), ("ev", 3, 0),
-)
+FLOPS = 2 * 2 * ROWS * WIDTH * WIDTH
 
 
 def tile_attention_prop_pa_kernel(tc, x, w1, b1, w2, b2, gamma, beta, out):
     nc = tc.nc
     with ExitStack() as ctx:
-        keep = ctx.enter_context(tc.tile_pool(name="keep", bufs=1))
-        ps = ctx.enter_context(tc.psum_pool(name="ps", bufs=1))
-        used = [0]
-
-        def new_bank(shape, name):
-            slot = used[0] % 8
-            used[0] = used[0] + 1
-            return ps.tile(shape, F32, tag="bank%d" % slot, name=name)
-
+        sbuf = ctx.enter_context(tc.tile_pool(name="sbuf", bufs=1))
+        psum = ctx.enter_context(tc.psum_pool(name="psum", bufs=1))
         ctx.enter_context(tc.manual_schedule())
-        T = {}
 
-        vb1 = keep.tile([P, P], BF16, name="vb1")
-        nc.vector.memset(vb1[:], 0.0)
-        vr = keep.tile([P, P], BF16, name="vr")
-        nc.vector.memset(vr[:], 0.0)
-        one = keep.tile([P, 1], F32, name="one")
+        banks_taken = [0]
+
+        def next_bank(shape, name):
+            tag = "bank%d" % (banks_taken[0] % BANKS)
+            banks_taken[0] = banks_taken[0] + 1
+            return psum.tile(shape, F32, tag=tag, name=name)
+
+        b1_rows = sbuf.tile([P, P], BF16, name="b1_rows")
+        nc.vector.memset(b1_rows[:], 0.0)
+        rest_rows = sbuf.tile([P, P], BF16, name="rest_rows")
+        nc.vector.memset(rest_rows[:], 0.0)
+        one = sbuf.tile([P, 1], F32, name="one")
         nc.vector.memset(one[:], 1.0)
-        nc.scalar.dma_start(out=vb1[0:4, :], in_=b1.rearrange("(t p) -> t p", p=P))
-        warm = keep.tile([P, 1], F32, name="warm")
-        nc.scalar.activation(out=warm[:], in_=one[:], func=ACT.Abs_reciprocal_sqrt)
-        ident = keep.tile([P, P], F32, name="ident")
-        make_identity(nc, ident[:])
-        for r, vec in enumerate((b2, gamma, beta)):
-            nc.gpsimd.dma_start(out=vr[4 * r : 4 * r + 4, :], in_=vec.rearrange("(t p) -> t p", p=P))
+        nc.scalar.dma_start(out=b1_rows[0:PACK, :], in_=b1.rearrange("(t p) -> t p", p=P))
+        table_warmer = sbuf.tile([P, 1], F32, name="table_warmer")
+        nc.scalar.activation(out=table_warmer[:], in_=one[:], func=ACT.Abs_reciprocal_sqrt)
+        identity = sbuf.tile([P, P], F32, name="identity")
+        make_identity(nc, identity[:])
+        for r, values in enumerate((b2, gamma, beta)):
+            nc.gpsimd.dma_start(
+                out=rest_rows[PACK * r : PACK * (r + 1), :], in_=values.rearrange("(t p) -> t p", p=P)
+            )
 
-        w1_view = w1.rearrange("(p j) f -> p j f", j=4)
-        x_view = x.rearrange("(i c) k -> i (c k)", c=8)
-        wsb = {}
-        x_sb = {}
+        x_view = x.rearrange("(i c) k -> i (c k)", c=GROUPS)
+        w_view = {
+            "w1a": w1.rearrange("(p t) f -> p t f", t=PACK)[:, :, 0:W1_PART],
+            "w1b": w1.rearrange("(p t) f -> p t f", t=PACK)[:, :, W1_PART:WIDTH],
+            "w2": w2.rearrange("(t p) f -> p t f", p=P),
+        }
+        w_width = {"w1a": W1_PART, "w1b": WIDTH - W1_PART, "w2": WIDTH}
+        x_raw = {}
+        w_raw = {}
 
-        def load_w1(nm, lo):
-            wsb[nm] = keep.tile([P, 4, 256], BF16, name="sb_" + nm)
-            nc.sync.dma_start(out=wsb[nm][:], in_=w1_view[:, :, lo : lo + 256])
+        def load_x(piece):
+            x_raw[piece] = sbuf.tile([P, 2 * WIDTH], BF16, name="x_raw%d" % piece)
+            nc.sync.dma_start(out=x_raw[piece][:], in_=x_view[:, 2 * WIDTH * piece : 2 * WIDTH * (piece + 1)])
 
-        def load_x(j):
-            x_sb[j] = keep.tile([P, 1024], BF16, name="x_sb%d" % j)
-            nc.sync.dma_start(out=x_sb[j][:], in_=x_view[:, 1024 * j : 1024 * (j + 1)])
+        def load_w(part):
+            w_raw[part] = sbuf.tile([P, PACK, w_width[part]], BF16, name="raw_" + part)
+            nc.sync.dma_start(out=w_raw[part][:], in_=w_view[part])
 
         load_x(0)
+        load_w("w1a")
         load_x(1)
-        load_w1("w1a", 0)
+        load_w("w1b")
         load_x(2)
-        load_w1("w1b", 256)
-        wsb["w2"] = keep.tile([P, 4, F], BF16, name="sb_w2")
-        nc.sync.dma_start(out=wsb["w2"][:], in_=w2.rearrange("(t p) f -> p t f", p=P))
+        load_w("w2")
         load_x(3)
 
-        w1q = keep.tile([P, F], U32, align_bytes=64, name="w1q")
-        w1s = keep.tile([P, F], U8, align_bytes=64, name="w1s")
-        w2q = keep.tile([P, F], U32, align_bytes=64, name="w2q")
-        w2s = keep.tile([P, F], U8, align_bytes=64, name="w2s")
-        xq = keep.tile([P, NQ], U32, align_bytes=64, name="xq")
-        xs = keep.tile([P, NQ], U8, align_bytes=64, name="xs")
-        hq = keep.tile([P, NQ], U32, align_bytes=64, name="hq")
-        hs = keep.tile([P, NQ], U8, align_bytes=64, name="hs")
-        wdst = {"w1a": (w1q, w1s, 0, 256), "w1b": (w1q, w1s, 256, 256), "w2": (w2q, w2s, 0, 512)}
-        b1T = keep.tile([P, 4], F32, name="b1T")
-        rT = keep.tile([P, 12], F32, name="rT")
-        b2s = keep.tile([P, 4], F32, name="b2s")
-        gpair = keep.tile([P, 4, 2], F32, name="gpair")
-        negc = keep.tile([P, 4], F32, name="negc")
-        out_view = out.rearrange("(i c) f -> i c f", c=8)
+        w1_words = sbuf.tile([P, WIDTH], U32, align_bytes=64, name="w1_words")
+        w1_plane = sbuf.tile([P, WIDTH], U8, align_bytes=64, name="w1_plane")
+        w2_words = sbuf.tile([P, WIDTH], U32, align_bytes=64, name="w2_words")
+        w2_plane = sbuf.tile([P, WIDTH], U8, align_bytes=64, name="w2_plane")
+        x_words = sbuf.tile([P, ROWS], U32, align_bytes=64, name="x_words")
+        x_plane = sbuf.tile([P, ROWS], U8, align_bytes=64, name="x_plane")
+        h1_words = sbuf.tile([P, ROWS], U32, align_bytes=64, name="h1_words")
+        h1_plane = sbuf.tile([P, ROWS], U8, align_bytes=64, name="h1_plane")
+        w_packed = {
+            "w1a": (w1_words[:, 0:W1_PART], w1_plane[:, 0:W1_PART]),
+            "w1b": (w1_words[:, W1_PART:WIDTH], w1_plane[:, W1_PART:WIDTH]),
+            "w2": (w2_words[:], w2_plane[:]),
+        }
 
-        def step(tok):
-            k = tok[0]
-            if k == "vf1":
-                T["vf1"] = keep.tile([P, P], F32, name="vf1")
-                nc.vector.tensor_copy(out=T["vf1"][:], in_=vb1[:])
-            elif k == "vT1":
-                T["vp1"] = new_bank([P, P], "vp1")
-                nc.tensor.transpose(T["vp1"][:], T["vf1"][:], ident[:])
-            elif k == "vc1":
-                nc.vector.tensor_copy(out=b1T[:], in_=T["vp1"][:, 0:4])
-            elif k == "vf2":
-                T["vf2"] = keep.tile([P, P], F32, name="vf2")
-                nc.scalar.copy(out=T["vf2"][:], in_=vr[:])
-            elif k == "vT2":
-                T["vp2"] = new_bank([P, P], "vp2")
-                nc.tensor.transpose(T["vp2"][:], T["vf2"][:], ident[:])
-            elif k == "vc2":
-                nc.scalar.copy(out=rT[:], in_=T["vp2"][:, 0:12])
-                nc.scalar.mul(out=b2s[:], in_=rT[:, 0:4], mul=1.0 - SLOPE)
-                nc.scalar.copy(out=gpair[:, :, 0], in_=rT[:, 4:8])
-                nc.scalar.mul(out=gpair[:, :, 1], in_=rT[:, 4:8], mul=-1.0)
-                T["posc"] = keep.tile([P, 4], F32, name="posc")
-                nc.scalar.activation(out=T["posc"][:], in_=b2s[:], func=ACT.Relu)
-                nc.scalar.mul(out=negc[:], in_=T["posc"][:], mul=-1.0)
-            elif k == "rg":
-                nm = tok[1]
-                width = wdst[nm][3]
-                g = keep.tile([P, width, 4], BF16, align_bytes=64, name="g_" + nm)
-                T["g_" + nm] = g
-                dst = g[:].rearrange("p (c i) t -> p c t i", i=4)
-                src = wsb[nm][:].rearrange("p t (c i) -> p c t i", i=4)
-                if tok[2] == "V":
-                    nc.vector.tensor_copy(out=dst, in_=src)
-                else:
-                    nc.scalar.copy(out=dst, in_=src)
-            elif k == "qw":
-                nm = tok[1]
-                codes, scales, lo, width = wdst[nm]
-                nc.vector.quantize_mx(
-                    out=codes[:, lo : lo + width].bitcast(FP8X4),
-                    scales=scales[:, lo : lo + width],
-                    in_=T["g_" + nm][:].rearrange("p f t -> p (f t)"),
-                )
-            elif k == "xT":
-                j = tok[1]
-                xt = new_bank([P, 2, 2, P], "xt%d" % j)
-                T["xt", j] = xt
-                xw = x_sb[j][:].bitcast(F32).rearrange("i (cc w u) -> i cc u w", cc=2, u=2)
-                for cc in range(2):
-                    for u in range(2):
-                        nc.tensor.transpose(xt[:, cc, u, :], xw[:, cc, u, :], ident[:])
-            elif k == "xc":
-                j = tok[1]
-                xg = keep.tile([P, 1024], BF16, align_bytes=64, name="xg%d" % j)
-                T["xg", j] = xg
-                dst = xg[:].bitcast(F32).rearrange("p (cc i u) -> p cc i u", cc=2, u=2)
-                src = T["xt", j][:].rearrange("p cc u i -> p cc i u")
-                if tok[2] == "S":
-                    nc.scalar.copy(out=dst, in_=src)
-                else:
-                    nc.vector.tensor_copy(out=dst, in_=src)
-            elif k == "xq":
-                j = tok[1]
-                sl = slice(256 * j, 256 * (j + 1))
-                nc.vector.quantize_mx(out=xq[:, sl].bitcast(FP8X4), scales=xs[:, sl], in_=T["xg", j][:])
-            elif k == "m1":
-                pi = tok[1]
-                sl = slice(256 * pi, 256 * (pi + 1))
-                if ("v", pi) not in T:
-                    T["v", pi] = keep.tile([P, 4, 256], F32, name="v%d" % pi)
-                for tp in (tok[2],):
-                    bank = new_bank([P, 2, 256], "l1_%d_%d" % (pi, tp))
-                    T["l1", pi, tp] = bank
-                    for e in range(2):
-                        t = 2 * tp + e
-                        nc.tensor.matmul_mx(
-                            out=bank[:, e, :],
-                            lhsT=w1q[:, P * t : P * (t + 1)].bitcast(FP8X4),
-                            lhsT_scale=w1s[:, P * t : P * (t + 1)],
-                            rhs=xq[:, sl].bitcast(FP8X4),
-                            rhs_scale=xs[:, sl],
-                            start=True,
-                            stop=True,
-                        )
-            elif k == "s1":
-                pi, t = tok[1], tok[2]
-                nc.scalar.activation(
-                    out=T["v", pi][:, t, :],
-                    in_=T["l1", pi, t // 2][:, t % 2, :],
-                    func=ACT.Identity,
-                    bias=b1T[:, t : t + 1],
-                    scale=1.0,
-                )
-            elif k == "lk":
-                pi = tok[1]
-                hg = keep.tile([P, 256, 4], BF16, align_bytes=64, name="hg%d" % pi)
-                T["hg", pi] = hg
-                vp = T["v", pi][:].rearrange("p t n -> p n t")
-                nc.vector.scalar_tensor_tensor(out=hg[:], in0=vp, scalar=SLOPE, in1=vp, op0=ALU.mult, op1=ALU.max)
-            elif k == "hq":
-                pi = tok[1]
-                sl = slice(256 * pi, 256 * (pi + 1))
-                nc.vector.quantize_mx(
-                    out=hq[:, sl].bitcast(FP8X4), scales=hs[:, sl], in_=T["hg", pi][:].rearrange("p n t -> p (n t)")
-                )
-            elif k == "m2":
-                c, h = tok[1], tok[2]
-                fs = slice(P * c, P * (c + 1))
-                cols = slice(512 * h, 512 * (h + 1))
-                p2 = new_bank([P, 512], "l2_%d_%d" % (c, h))
-                T["l2", c, h] = p2
+        w_grouped = {}
+
+        def regroup_w(part):
+            w_grouped[part] = sbuf.tile([P, w_width[part], PACK], BF16, align_bytes=64, name="grouped_" + part)
+            nc.vector.tensor_copy(
+                out=w_grouped[part][:].rearrange("p (b r) t -> p b t r", r=4),
+                in_=w_raw[part][:].rearrange("p t (b r) -> p b t r", r=4),
+            )
+
+        def quantise_w(part):
+            words, plane = w_packed[part]
+            nc.vector.quantize_mx(
+                out=words.bitcast(FP8X4), scales=plane, in_=w_grouped[part][:].rearrange("p f t -> p (f t)")
+            )
+
+        x_bank = {}
+        x_grouped = {}
+
+        def transpose_x(piece):
+            x_bank[piece] = next_bank([P, 2, 2, P], "x_bank%d" % piece)
+            pairs = x_raw[piece][:].bitcast(F32).rearrange("i (c p u) -> i c u p", c=2, u=2)
+            for c in range(2):
+                for u in range(2):
+                    nc.tensor.transpose(x_bank[piece][:, c, u, :], pairs[:, c, u, :], identity[:])
+
+        def copy_x(piece):
+            x_grouped[piece] = sbuf.tile([P, PACK * PIECE], BF16, align_bytes=64, name="x_grouped%d" % piece)
+            nc.scalar.copy(
+                out=x_grouped[piece][:].bitcast(F32).rearrange("p (c i u) -> p c i u", c=2, u=2),
+                in_=x_bank[piece][:].rearrange("p c u i -> p c i u"),
+            )
+
+        def piece_columns(piece):
+            return slice(PIECE * piece, PIECE * (piece + 1))
+
+        def quantise_x(piece):
+            cols = piece_columns(piece)
+            nc.vector.quantize_mx(
+                out=x_words[:, cols].bitcast(FP8X4), scales=x_plane[:, cols], in_=x_grouped[piece][:]
+            )
+
+        b1_f32 = sbuf.tile([P, P], F32, name="b1_f32")
+        b1_col = sbuf.tile([P, PACK], F32, name="b1_col")
+        vector_bank = {}
+
+        def cast_b1():
+            nc.vector.tensor_copy(out=b1_f32[:], in_=b1_rows[:])
+
+        def transpose_b1():
+            vector_bank["b1"] = next_bank([P, P], "b1_bank")
+            nc.tensor.transpose(vector_bank["b1"][:], b1_f32[:], identity[:])
+
+        def copy_b1():
+            nc.vector.tensor_copy(out=b1_col[:], in_=vector_bank["b1"][:, 0:PACK])
+
+        rest_f32 = sbuf.tile([P, P], F32, name="rest_f32")
+        rest_col = sbuf.tile([P, 3 * PACK], F32, name="rest_col")
+        b2_most = sbuf.tile([P, PACK], F32, name="b2_most")
+        centre = sbuf.tile([P, PACK], F32, name="centre")
+        minus_centre = sbuf.tile([P, PACK], F32, name="minus_centre")
+        gamma_pair = sbuf.tile([P, PACK, 2], F32, name="gamma_pair")
+
+        def beta_col(chunk):
+            return rest_col[:, 2 * PACK + chunk : 2 * PACK + chunk + 1]
+
+        def cast_rest():
+            nc.scalar.copy(out=rest_f32[:], in_=rest_rows[:])
+
+        def transpose_rest():
+            vector_bank["rest"] = next_bank([P, P], "rest_bank")
+            nc.tensor.transpose(vector_bank["rest"][:], rest_f32[:], identity[:])
+
+        def derive_rest():
+            nc.scalar.copy(out=rest_col[:], in_=vector_bank["rest"][:, 0 : 3 * PACK])
+            nc.scalar.mul(out=b2_most[:], in_=rest_col[:, 0:PACK], mul=1.0 - SLOPE)
+            nc.scalar.copy(out=gamma_pair[:, :, 0], in_=rest_col[:, PACK : 2 * PACK])
+            nc.scalar.mul(out=gamma_pair[:, :, 1], in_=rest_col[:, PACK : 2 * PACK], mul=-1.0)
+            nc.scalar.activation(out=centre[:], in_=b2_most[:], func=ACT.Relu)
+            nc.scalar.mul(out=minus_centre[:], in_=centre[:], mul=-1.0)
+
+        l1_bank = {}
+        v = {}
+        h1_grouped = {}
+
+        def layer1(piece, pair):
+            cols = piece_columns(piece)
+            l1_bank[piece, pair] = next_bank([P, 2, PIECE], "l1_bank%d_%d" % (piece, pair))
+            for e in range(2):
+                features = slice(P * (2 * pair + e), P * (2 * pair + e + 1))
                 nc.tensor.matmul_mx(
-                    out=p2[:],
-                    lhsT=w2q[:, fs].bitcast(FP8X4),
-                    lhsT_scale=w2s[:, fs],
-                    rhs=hq[:, cols].bitcast(FP8X4),
-                    rhs_scale=hs[:, cols],
+                    out=l1_bank[piece, pair][:, e, :],
+                    lhsT=w1_words[:, features].bitcast(FP8X4),
+                    lhsT_scale=w1_plane[:, features],
+                    rhs=x_words[:, cols].bitcast(FP8X4),
+                    rhs_scale=x_plane[:, cols],
                     start=True,
                     stop=True,
                 )
-            elif k == "a0":
-                c, h = tok[1], tok[2]
-                T["a0", c, h] = keep.tile([P, 512], F32, name="a0_%d_%d" % (c, h))
-                if LEAK[c] == "G":
-                    nc.scalar.activation(
-                        out=T["a0", c, h][:], in_=T["l2", c, h][:], func=ACT.Identity, bias=rT[:, c : c + 1], scale=1.0
-                    )
-                else:
-                    nc.scalar.mul(out=T["a0", c, h][:], in_=T["l2", c, h][:], mul=SLOPE)
-            elif k == "st":
-                c, h = tok[1], tok[2]
-                if ("q", c) not in T:
-                    T["q", c] = keep.tile([P, NQ], F32, name="q%d" % c)
-                    if STAT[c] == "S":
-                        T["ssum", c] = keep.tile([P, 2], F32, name="ssum%d" % c)
-                        T["ssq", c] = keep.tile([P, 2], F32, name="ssq%d" % c)
-                    else:
-                        T["stats", c] = keep.tile([P, 2, 6], F32, name="stats%d" % c)
-                if LEAK[c] == "G":
-                    neg = keep.tile([P, 512], F32, name="neg_%d_%d" % (c, h))
-                    nc.gpsimd.tensor_scalar(
-                        out=neg[:], in0=T["a0", c, h][:], scalar1=SLOPE - 1.0, scalar2=0.0, op0=ALU.mult, op1=ALU.max
-                    )
-                    nc.gpsimd.tensor_tensor(
-                        out=T["q", c][:, 512 * h : 512 * (h + 1)], in0=T["a0", c, h][:], in1=neg[:], op=ALU.add
-                    )
-                else:
-                    nc.vector.scalar_tensor_tensor(
-                        out=T["q", c][:, 512 * h : 512 * (h + 1)],
-                        in0=T["l2", c, h][:],
-                        scalar=b2s[:, c : c + 1],
-                        in1=T["a0", c, h][:],
-                        op0=ALU.add,
-                        op1=ALU.max,
-                        accum_out=T["ssum", c][:, h : h + 1] if STAT[c] == "S" else None,
-                    )
-            elif k == "bn":
-                c, h = tok[1], tok[2]
-                if STAT[c] == "S":
-                    junk = keep.tile([P, 512], BF16, name="junk_%d_%d" % (c, h))
-                    nc.scalar.activation(
-                        out=junk[:],
-                        in_=T["q", c][:, 512 * h : 512 * (h + 1)],
-                        func=ACT.Square,
-                        bias=negc[:, c : c + 1],
-                        scale=1.0,
-                        accum_out=T["ssq", c][:, h : h + 1],
-                    )
-                else:
-                    nc.vector.bn_stats(out=T["stats", c][:, h, :], in_=T["q", c][:, 512 * h : 512 * (h + 1)])
-            elif k == "ag":
-                c = tok[1]
-                T["mv", c] = keep.tile([P, 2], F32, name="mv%d" % c)
-                if STAT[c] == "S":
-                    ms = keep.tile([P, 2], F32, name="ms%d" % c)
-                    nc.gpsimd.tensor_scalar(
-                        out=T["mv", c][:, 0:1],
-                        in0=T["ssum", c][:, 0:1],
-                        scalar1=T["ssum", c][:, 1:2],
-                        scalar2=1.0 / NQ,
-                        op0=ALU.add,
-                        op1=ALU.mult,
-                    )
-                    nc.gpsimd.tensor_scalar(
-                        out=ms[:, 0:1],
-                        in0=T["ssq", c][:, 0:1],
-                        scalar1=T["ssq", c][:, 1:2],
-                        scalar2=1.0 / NQ,
-                        op0=ALU.add,
-                        op1=ALU.mult,
-                    )
-                    nc.gpsimd.tensor_scalar(
-                        out=ms[:, 1:2], in0=T["mv", c][:, 0:1], scalar1=negc[:, c : c + 1], scalar2=0.0, op0=ALU.add, op1=ALU.add
-                    )
-                    nc.gpsimd.tensor_scalar(
-                        out=T["mv", c][:, 1:2],
-                        in0=ms[:, 1:2],
-                        scalar1=ms[:, 1:2],
-                        scalar2=ms[:, 0:1],
-                        op0=ALU.mult,
-                        op1=ALU.subtract,
-                    )
-                else:
-                    nc.vector.bn_aggr(out=T["mv", c][:], in_=T["stats", c][:].rearrange("p a b -> p (a b)"))
-            elif k == "rs":
-                c = tok[1]
-                T["rstd", c] = keep.tile([P, 1], F32, name="rstd%d" % c)
+
+        def add_b1(piece):
+            v[piece] = sbuf.tile([P, PACK, PIECE], F32, name="v%d" % piece)
+            for t in range(PACK):
                 nc.scalar.activation(
-                    out=T["rstd", c][:],
-                    in_=T["mv", c][:, 1:2],
-                    func=ACT.Abs_reciprocal_sqrt,
-                    bias=EPS,
-                    scale=-1.0 if STAT[c] == "S" else 1.0,
+                    out=v[piece][:, t, :],
+                    in_=l1_bank[piece, t // 2][:, t % 2, :],
+                    func=ACT.Identity,
+                    bias=b1_col[:, t : t + 1],
+                    scale=1.0,
                 )
-            elif k == "ab":
-                c = tok[1]
-                T["ab", c] = keep.tile([P, 2], F32, name="ab%d" % c)
-                T["sh", c] = keep.tile([P, 1], F32, name="sh%d" % c)
-                e = nc.gpsimd if ABENG[c] == "G" else nc.vector
-                e.tensor_scalar(
-                    out=T["ab", c][:], in0=gpair[:, c, :], scalar1=T["rstd", c][:, 0:1], scalar2=0.0, op0=ALU.mult, op1=ALU.add
+
+        def leaky1(piece):
+            h1_grouped[piece] = sbuf.tile([P, PIECE, PACK], BF16, align_bytes=64, name="h1_grouped%d" % piece)
+            by_row = v[piece][:].rearrange("p t n -> p n t")
+            nc.vector.scalar_tensor_tensor(
+                out=h1_grouped[piece][:], in0=by_row, scalar=SLOPE, in1=by_row, op0=ALU.mult, op1=ALU.max
+            )
+
+        def quantise_h1(piece):
+            cols = piece_columns(piece)
+            nc.vector.quantize_mx(
+                out=h1_words[:, cols].bitcast(FP8X4),
+                scales=h1_plane[:, cols],
+                in_=h1_grouped[piece][:].rearrange("p n t -> p (n t)"),
+            )
+
+        def half_columns(half):
+            return slice(HALF * half, HALF * (half + 1))
+
+        l2_bank = {}
+        sloped = {}
+        q = {}
+
+        def layer2(chunk, half):
+            features = slice(P * chunk, P * (chunk + 1))
+            cols = half_columns(half)
+            l2_bank[chunk, half] = next_bank([P, HALF], "l2_bank%d_%d" % (chunk, half))
+            nc.tensor.matmul_mx(
+                out=l2_bank[chunk, half][:],
+                lhsT=w2_words[:, features].bitcast(FP8X4),
+                lhsT_scale=w2_plane[:, features],
+                rhs=h1_words[:, cols].bitcast(FP8X4),
+                rhs_scale=h1_plane[:, cols],
+                start=True,
+                stop=True,
+            )
+
+        def slope2(chunk, half):
+            sloped[chunk, half] = sbuf.tile([P, HALF], F32, name="sloped%d_%d" % (chunk, half))
+            nc.scalar.mul(out=sloped[chunk, half][:], in_=l2_bank[chunk, half][:], mul=SLOPE)
+
+        def leaky2(chunk, half, row_sum=None):
+            if chunk not in q:
+                q[chunk] = sbuf.tile([P, ROWS], F32, name="q%d" % chunk)
+            nc.vector.scalar_tensor_tensor(
+                out=q[chunk][:, half_columns(half)],
+                in0=l2_bank[chunk, half][:],
+                scalar=b2_most[:, chunk : chunk + 1],
+                in1=sloped[chunk, half][:],
+                op0=ALU.add,
+                op1=ALU.max,
+                accum_out=row_sum,
+            )
+
+        half_stats = {}
+        moments = {}
+
+        def stats_on_vector(chunk, half):
+            if chunk not in half_stats:
+                half_stats[chunk] = sbuf.tile([P, 2, 6], F32, name="half_stats%d" % chunk)
+            nc.vector.bn_stats(out=half_stats[chunk][:, half, :], in_=q[chunk][:, half_columns(half)])
+
+        def moments_on_vector(chunk):
+            moments[chunk] = sbuf.tile([P, 2], F32, name="moments%d" % chunk)
+            nc.vector.bn_aggr(out=moments[chunk][:], in_=half_stats[chunk][:].rearrange("p h s -> p (h s)"))
+
+        sums = sbuf.tile([P, 2], F32, name="sums")
+        squares = sbuf.tile([P, 2], F32, name="squares")
+
+        def squares_on_scalar(chunk, half):
+            unused = sbuf.tile([P, HALF], BF16, name="unused%d" % half)
+            nc.scalar.activation(
+                out=unused[:],
+                in_=q[chunk][:, half_columns(half)],
+                func=ACT.Square,
+                bias=minus_centre[:, chunk : chunk + 1],
+                scale=1.0,
+                accum_out=squares[:, half : half + 1],
+            )
+
+        def moments_on_gpsimd(chunk):
+            moments[chunk] = sbuf.tile([P, 2], F32, name="moments%d" % chunk)
+            work = sbuf.tile([P, 2], F32, name="moments_work")
+            nc.gpsimd.tensor_scalar(
+                out=moments[chunk][:, 0:1],
+                in0=sums[:, 0:1],
+                scalar1=sums[:, 1:2],
+                scalar2=1.0 / ROWS,
+                op0=ALU.add,
+                op1=ALU.mult,
+            )
+            nc.gpsimd.tensor_scalar(
+                out=work[:, 0:1],
+                in0=squares[:, 0:1],
+                scalar1=squares[:, 1:2],
+                scalar2=1.0 / ROWS,
+                op0=ALU.add,
+                op1=ALU.mult,
+            )
+            nc.gpsimd.tensor_scalar(
+                out=work[:, 1:2],
+                in0=moments[chunk][:, 0:1],
+                scalar1=minus_centre[:, chunk : chunk + 1],
+                scalar2=0.0,
+                op0=ALU.add,
+                op1=ALU.add,
+            )
+            nc.gpsimd.tensor_scalar(
+                out=moments[chunk][:, 1:2],
+                in0=work[:, 1:2],
+                scalar1=work[:, 1:2],
+                scalar2=work[:, 0:1],
+                op0=ALU.mult,
+                op1=ALU.subtract,
+            )
+
+        inverse_deviation = {}
+        gain = {}
+        shift = {}
+
+        def invert_deviation(chunk, variance_sign):
+            inverse_deviation[chunk] = sbuf.tile([P, 1], F32, name="inverse_deviation%d" % chunk)
+            nc.scalar.activation(
+                out=inverse_deviation[chunk][:],
+                in_=moments[chunk][:, 1:2],
+                func=ACT.Abs_reciprocal_sqrt,
+                bias=EPS,
+                scale=variance_sign,
+            )
+
+        def gain_and_shift(chunk, engine):
+            gain[chunk] = sbuf.tile([P, 2], F32, name="gain%d" % chunk)
+            shift[chunk] = sbuf.tile([P, 1], F32, name="shift%d" % chunk)
+            engine.tensor_scalar(
+                out=gain[chunk][:],
+                in0=gamma_pair[:, chunk, :],
+                scalar1=inverse_deviation[chunk][:, 0:1],
+                scalar2=0.0,
+                op0=ALU.mult,
+                op1=ALU.add,
+            )
+            engine.tensor_scalar(
+                out=shift[chunk][:],
+                in0=moments[chunk][:, 0:1],
+                scalar1=gain[chunk][:, 1:2],
+                scalar2=beta_col(chunk),
+                op0=ALU.mult,
+                op1=ALU.add,
+            )
+
+        y = {}
+
+        def normalise(chunk, half, engine):
+            if chunk not in y:
+                y[chunk] = sbuf.tile([P, ROWS], F32, name="y%d" % chunk)
+            cols = half_columns(half)
+            if engine is nc.scalar:
+                engine.activation(
+                    out=y[chunk][:, cols],
+                    in_=q[chunk][:, cols],
+                    func=ACT.Identity,
+                    bias=shift[chunk][:, 0:1],
+                    scale=gain[chunk][:, 0:1],
                 )
-                e.tensor_scalar(
-                    out=T["sh", c][:],
-                    in0=T["mv", c][:, 0:1],
-                    scalar1=T["ab", c][:, 1:2],
-                    scalar2=rT[:, 8 + c : 9 + c],
+            else:
+                engine.tensor_scalar(
+                    out=y[chunk][:, cols],
+                    in0=q[chunk][:, cols],
+                    scalar1=gain[chunk][:, 0:1],
+                    scalar2=shift[chunk][:, 0:1],
                     op0=ALU.mult,
                     op1=ALU.add,
                 )
-            elif k == "nm":
-                c, h = tok[1], tok[2]
-                if ("y", c) not in T:
-                    T["y", c] = keep.tile([P, NQ], F32, name="y%d" % c)
-                cols = slice(512 * h, 512 * (h + 1))
-                eng = NORM[c][h]
-                if eng == "S":
-                    nc.scalar.activation(
-                        out=T["y", c][:, cols],
-                        in_=T["q", c][:, cols],
-                        func=ACT.Identity,
-                        bias=T["sh", c][:, 0:1],
-                        scale=T["ab", c][:, 0:1],
-                    )
-                else:
-                    e = nc.gpsimd if eng == "G" else nc.vector
-                    e.tensor_scalar(
-                        out=T["y", c][:, cols],
-                        in0=T["q", c][:, cols],
-                        scalar1=T["ab", c][:, 0:1],
-                        scalar2=T["sh", c][:, 0:1],
-                        op0=ALU.mult,
-                        op1=ALU.add,
-                    )
-            elif k == "oT":
-                c, h = tok[1], tok[2]
-                ot = new_bank([P, 4, P], "ot_%d_%d" % (c, h))
-                T["ot", c, h] = ot
-                for cc in range(4):
-                    col = P * (4 * h + cc)
-                    nc.tensor.transpose(ot[:, cc, :], T["y", c][:, col : col + P], ident[:])
-            elif k == "ev":
-                c, h = tok[1], tok[2]
-                o_sb = keep.tile([P, 4, P], F32, name="o_%d_%d" % (c, h))
-                if EVAC[c][h] == "S":
-                    nc.scalar.copy(out=o_sb[:], in_=T["ot", c, h][:])
-                else:
-                    nc.vector.tensor_copy(out=o_sb[:], in_=T["ot", c, h][:])
-                nc.sync.dma_start(out=out_view[:, 4 * h : 4 * h + 4, P * c : P * (c + 1)], in_=o_sb[:])
-            else:
-                assert False, k
 
-        for tok in SCHED:
-            step(tok)
+        out_bank = {}
+        out_view = out.rearrange("(i c) f -> i c f", c=GROUPS)
+        groups_in_half = HALF // P
+
+        def transpose_out(chunk, half):
+            out_bank[chunk, half] = next_bank([P, groups_in_half, P], "out_bank%d_%d" % (chunk, half))
+            for c in range(groups_in_half):
+                first = HALF * half + P * c
+                nc.tensor.transpose(out_bank[chunk, half][:, c, :], y[chunk][:, first : first + P], identity[:])
+
+        def copy_and_store(chunk, half, engine):
+            rows = sbuf.tile([P, groups_in_half, P], F32, name="rows%d_%d" % (chunk, half))
+            if engine is nc.scalar:
+                engine.copy(out=rows[:], in_=out_bank[chunk, half][:])
+            else:
+                engine.tensor_copy(out=rows[:], in_=out_bank[chunk, half][:])
+            groups = slice(groups_in_half * half, groups_in_half * (half + 1))
+            nc.sync.dma_start(out=out_view[:, groups, P * chunk : P * (chunk + 1)], in_=rows[:])
+
+        scalar, vector, gpsimd = nc.scalar, nc.vector, nc.gpsimd
+
+        transpose_x(0)
+        copy_x(0)
+        regroup_w("w1a")
+        quantise_x(0)
+        quantise_w("w1a")
+        transpose_x(1)
+        copy_x(1)
+        cast_b1()
+        regroup_w("w1b")
+        quantise_x(1)
+        quantise_w("w1b")
+        transpose_x(2)
+        copy_x(2)
+        transpose_b1()
+        copy_b1()
+        regroup_w("w2")
+        quantise_x(2)
+        quantise_w("w2")
+
+        layer1(0, 0)
+        layer1(0, 1)
+        add_b1(0)
+        transpose_x(3)
+        copy_x(3)
+        leaky1(0)
+        quantise_x(3)
+        quantise_h1(0)
+        for piece in (1, 2, 3):
+            layer1(piece, 0)
+            layer1(piece, 1)
+            add_b1(piece)
+        leaky1(1)
+        quantise_h1(1)
+        leaky1(2)
+        leaky1(3)
+        quantise_h1(2)
+        quantise_h1(3)
+
+        cast_rest()
+        layer2(0, 0)
+        layer2(1, 0)
+        transpose_rest()
+        slope2(0, 0)
+        derive_rest()
+        slope2(1, 0)
+        layer2(2, 0)
+        slope2(2, 0)
+        leaky2(0, 0)
+        leaky2(1, 0, row_sum=sums[:, 0:1])
+        stats_on_vector(0, 0)
+        layer2(0, 1)
+        layer2(1, 1)
+        slope2(0, 1)
+        slope2(1, 1)
+        leaky2(0, 1)
+        leaky2(1, 1, row_sum=sums[:, 1:2])
+        stats_on_vector(0, 1)
+        squares_on_scalar(1, 0)
+        layer2(2, 1)
+        slope2(2, 1)
+        squares_on_scalar(1, 1)
+        leaky2(2, 0)
+        moments_on_vector(0)
+        leaky2(2, 1)
+        moments_on_gpsimd(1)
+        invert_deviation(0, 1.0)
+        gain_and_shift(0, vector)
+        stats_on_vector(2, 0)
+        stats_on_vector(2, 1)
+        layer2(3, 0)
+        slope2(3, 0)
+        normalise(0, 0, scalar)
+        normalise(0, 1, gpsimd)
+        invert_deviation(1, -1.0)
+        gain_and_shift(1, vector)
+        layer2(3, 1)
+        slope2(3, 1)
+        normalise(1, 0, scalar)
+        normalise(1, 1, gpsimd)
+        moments_on_vector(2)
+        leaky2(3, 0)
+        leaky2(3, 1)
+        invert_deviation(2, 1.0)
+        gain_and_shift(2, gpsimd)
+        stats_on_vector(3, 0)
+        stats_on_vector(3, 1)
+
+        for chunk in (0, 1):
+            for half in (0, 1):
+                transpose_out(chunk, half)
+        copy_and_store(0, 0, scalar)
+        copy_and_store(0, 1, scalar)
+        copy_and_store(1, 0, scalar)
+        normalise(2, 0, gpsimd)
+        normalise(2, 1, vector)
+        moments_on_vector(3)
+        copy_and_store(1, 1, vector)
+        invert_deviation(3, 1.0)
+        gain_and_shift(3, vector)
+        transpose_out(2, 0)
+        transpose_out(2, 1)
+        copy_and_store(2, 0, scalar)
+        copy_and_store(2, 1, scalar)
+        normalise(3, 0, vector)
+        normalise(3, 1, vector)
+        transpose_out(3, 0)
+        transpose_out(3, 1)
+        copy_and_store(3, 0, vector)
+        copy_and_store(3, 1, scalar)

@@ -15,10 +15,13 @@ P = 128
 ROWS = 1024
 WIDTH = 512
 PACK = 4
-GROUPS = ROWS // P
+STRIPES = ROWS // P
 PIECE = 256
-W1_PART = 256
 HALF = 512
+HALVES = ROWS // HALF
+W1_PART = 256
+RUN = 4
+BN_STATS_SIZE = 6
 BANKS = 8
 EPS = 1e-5
 SLOPE = 0.01
@@ -56,7 +59,9 @@ def tile_attention_prop_pa_kernel(tc, x, w1, b1, w2, b2, gamma, beta, out):
                 out=rest_rows[PACK * r : PACK * (r + 1), :], in_=values.rearrange("(t p) -> t p", p=P)
             )
 
-        x_view = x.rearrange("(i c) k -> i (c k)", c=GROUPS)
+        x_view = x.rearrange("(i c) k -> i (c k)", c=STRIPES)
+        stripes_in_piece = PIECE // P
+        x_share = stripes_in_piece * WIDTH
         w_view = {
             "w1a": w1.rearrange("(p t) f -> p t f", t=PACK)[:, :, 0:W1_PART],
             "w1b": w1.rearrange("(p t) f -> p t f", t=PACK)[:, :, W1_PART:WIDTH],
@@ -67,8 +72,8 @@ def tile_attention_prop_pa_kernel(tc, x, w1, b1, w2, b2, gamma, beta, out):
         w_raw = {}
 
         def load_x(piece):
-            x_raw[piece] = sbuf.tile([P, 2 * WIDTH], BF16, name="x_raw%d" % piece)
-            nc.sync.dma_start(out=x_raw[piece][:], in_=x_view[:, 2 * WIDTH * piece : 2 * WIDTH * (piece + 1)])
+            x_raw[piece] = sbuf.tile([P, x_share], BF16, name="x_raw%d" % piece)
+            nc.sync.dma_start(out=x_raw[piece][:], in_=x_view[:, x_share * piece : x_share * (piece + 1)])
 
         def load_w(part):
             w_raw[part] = sbuf.tile([P, PACK, w_width[part]], BF16, name="raw_" + part)
@@ -101,8 +106,8 @@ def tile_attention_prop_pa_kernel(tc, x, w1, b1, w2, b2, gamma, beta, out):
         def regroup_w(part):
             w_grouped[part] = sbuf.tile([P, w_width[part], PACK], BF16, align_bytes=64, name="grouped_" + part)
             nc.vector.tensor_copy(
-                out=w_grouped[part][:].rearrange("p (b r) t -> p b t r", r=4),
-                in_=w_raw[part][:].rearrange("p t (b r) -> p b t r", r=4),
+                out=w_grouped[part][:].rearrange("p (b r) t -> p b t r", r=RUN),
+                in_=w_raw[part][:].rearrange("p t (b r) -> p b t r", r=RUN),
             )
 
         def quantise_w(part):
@@ -115,16 +120,16 @@ def tile_attention_prop_pa_kernel(tc, x, w1, b1, w2, b2, gamma, beta, out):
         x_grouped = {}
 
         def transpose_x(piece):
-            x_bank[piece] = next_bank([P, 2, 2, P], "x_bank%d" % piece)
-            pairs = x_raw[piece][:].bitcast(F32).rearrange("i (c p u) -> i c u p", c=2, u=2)
-            for c in range(2):
+            x_bank[piece] = next_bank([P, stripes_in_piece, 2, P], "x_bank%d" % piece)
+            x_as_f32 = x_raw[piece][:].bitcast(F32).rearrange("i (c p u) -> i c u p", c=stripes_in_piece, u=2)
+            for c in range(stripes_in_piece):
                 for u in range(2):
-                    nc.tensor.transpose(x_bank[piece][:, c, u, :], pairs[:, c, u, :], identity[:])
+                    nc.tensor.transpose(x_bank[piece][:, c, u, :], x_as_f32[:, c, u, :], identity[:])
 
         def copy_x(piece):
             x_grouped[piece] = sbuf.tile([P, PACK * PIECE], BF16, align_bytes=64, name="x_grouped%d" % piece)
             nc.scalar.copy(
-                out=x_grouped[piece][:].bitcast(F32).rearrange("p (c i u) -> p c i u", c=2, u=2),
+                out=x_grouped[piece][:].bitcast(F32).rearrange("p (c i u) -> p c i u", c=stripes_in_piece, u=2),
                 in_=x_bank[piece][:].rearrange("p c u i -> p c i u"),
             )
 
@@ -139,24 +144,24 @@ def tile_attention_prop_pa_kernel(tc, x, w1, b1, w2, b2, gamma, beta, out):
 
         b1_f32 = sbuf.tile([P, P], F32, name="b1_f32")
         b1_col = sbuf.tile([P, PACK], F32, name="b1_col")
-        vector_bank = {}
+        small_bank = {}
 
         def cast_b1():
             nc.vector.tensor_copy(out=b1_f32[:], in_=b1_rows[:])
 
         def transpose_b1():
-            vector_bank["b1"] = next_bank([P, P], "b1_bank")
-            nc.tensor.transpose(vector_bank["b1"][:], b1_f32[:], identity[:])
+            small_bank["b1"] = next_bank([P, P], "b1_bank")
+            nc.tensor.transpose(small_bank["b1"][:], b1_f32[:], identity[:])
 
         def copy_b1():
-            nc.vector.tensor_copy(out=b1_col[:], in_=vector_bank["b1"][:, 0:PACK])
+            nc.vector.tensor_copy(out=b1_col[:], in_=small_bank["b1"][:, 0:PACK])
 
         rest_f32 = sbuf.tile([P, P], F32, name="rest_f32")
         rest_col = sbuf.tile([P, 3 * PACK], F32, name="rest_col")
         b2_most = sbuf.tile([P, PACK], F32, name="b2_most")
         centre = sbuf.tile([P, PACK], F32, name="centre")
         minus_centre = sbuf.tile([P, PACK], F32, name="minus_centre")
-        gamma_pair = sbuf.tile([P, PACK, 2], F32, name="gamma_pair")
+        gamma_signed = sbuf.tile([P, PACK, 2], F32, name="gamma_signed")
 
         def beta_col(chunk):
             return rest_col[:, 2 * PACK + chunk : 2 * PACK + chunk + 1]
@@ -165,14 +170,14 @@ def tile_attention_prop_pa_kernel(tc, x, w1, b1, w2, b2, gamma, beta, out):
             nc.scalar.copy(out=rest_f32[:], in_=rest_rows[:])
 
         def transpose_rest():
-            vector_bank["rest"] = next_bank([P, P], "rest_bank")
-            nc.tensor.transpose(vector_bank["rest"][:], rest_f32[:], identity[:])
+            small_bank["rest"] = next_bank([P, P], "rest_bank")
+            nc.tensor.transpose(small_bank["rest"][:], rest_f32[:], identity[:])
 
         def derive_rest():
-            nc.scalar.copy(out=rest_col[:], in_=vector_bank["rest"][:, 0 : 3 * PACK])
+            nc.scalar.copy(out=rest_col[:], in_=small_bank["rest"][:, 0 : 3 * PACK])
             nc.scalar.mul(out=b2_most[:], in_=rest_col[:, 0:PACK], mul=1.0 - SLOPE)
-            nc.scalar.copy(out=gamma_pair[:, :, 0], in_=rest_col[:, PACK : 2 * PACK])
-            nc.scalar.mul(out=gamma_pair[:, :, 1], in_=rest_col[:, PACK : 2 * PACK], mul=-1.0)
+            nc.scalar.copy(out=gamma_signed[:, :, 0], in_=rest_col[:, PACK : 2 * PACK])
+            nc.scalar.mul(out=gamma_signed[:, :, 1], in_=rest_col[:, PACK : 2 * PACK], mul=-1.0)
             nc.scalar.activation(out=centre[:], in_=b2_most[:], func=ACT.Relu)
             nc.scalar.mul(out=minus_centre[:], in_=centre[:], mul=-1.0)
 
@@ -264,15 +269,15 @@ def tile_attention_prop_pa_kernel(tc, x, w1, b1, w2, b2, gamma, beta, out):
 
         def stats_on_vector(chunk, half):
             if chunk not in half_stats:
-                half_stats[chunk] = sbuf.tile([P, 2, 6], F32, name="half_stats%d" % chunk)
+                half_stats[chunk] = sbuf.tile([P, HALVES, BN_STATS_SIZE], F32, name="half_stats%d" % chunk)
             nc.vector.bn_stats(out=half_stats[chunk][:, half, :], in_=q[chunk][:, half_columns(half)])
 
         def moments_on_vector(chunk):
             moments[chunk] = sbuf.tile([P, 2], F32, name="moments%d" % chunk)
             nc.vector.bn_aggr(out=moments[chunk][:], in_=half_stats[chunk][:].rearrange("p h s -> p (h s)"))
 
-        sums = sbuf.tile([P, 2], F32, name="sums")
-        squares = sbuf.tile([P, 2], F32, name="squares")
+        sums = sbuf.tile([P, HALVES], F32, name="sums")
+        squares = sbuf.tile([P, HALVES], F32, name="squares")
 
         def squares_on_scalar(chunk, half):
             unused = sbuf.tile([P, HALF], BF16, name="unused%d" % half)
@@ -340,7 +345,7 @@ def tile_attention_prop_pa_kernel(tc, x, w1, b1, w2, b2, gamma, beta, out):
             shift[chunk] = sbuf.tile([P, 1], F32, name="shift%d" % chunk)
             engine.tensor_scalar(
                 out=gain[chunk][:],
-                in0=gamma_pair[:, chunk, :],
+                in0=gamma_signed[:, chunk, :],
                 scalar1=inverse_deviation[chunk][:, 0:1],
                 scalar2=0.0,
                 op0=ALU.mult,
@@ -380,23 +385,23 @@ def tile_attention_prop_pa_kernel(tc, x, w1, b1, w2, b2, gamma, beta, out):
                 )
 
         out_bank = {}
-        out_view = out.rearrange("(i c) f -> i c f", c=GROUPS)
-        groups_in_half = HALF // P
+        out_view = out.rearrange("(i c) f -> i c f", c=STRIPES)
+        stripes_in_half = HALF // P
 
         def transpose_out(chunk, half):
-            out_bank[chunk, half] = next_bank([P, groups_in_half, P], "out_bank%d_%d" % (chunk, half))
-            for c in range(groups_in_half):
+            out_bank[chunk, half] = next_bank([P, stripes_in_half, P], "out_bank%d_%d" % (chunk, half))
+            for c in range(stripes_in_half):
                 first = HALF * half + P * c
                 nc.tensor.transpose(out_bank[chunk, half][:, c, :], y[chunk][:, first : first + P], identity[:])
 
         def copy_and_store(chunk, half, engine):
-            rows = sbuf.tile([P, groups_in_half, P], F32, name="rows%d_%d" % (chunk, half))
+            rows = sbuf.tile([P, stripes_in_half, P], F32, name="rows%d_%d" % (chunk, half))
             if engine is nc.scalar:
                 engine.copy(out=rows[:], in_=out_bank[chunk, half][:])
             else:
                 engine.tensor_copy(out=rows[:], in_=out_bank[chunk, half][:])
-            groups = slice(groups_in_half * half, groups_in_half * (half + 1))
-            nc.sync.dma_start(out=out_view[:, groups, P * chunk : P * (chunk + 1)], in_=rows[:])
+            stripes = slice(stripes_in_half * half, stripes_in_half * (half + 1))
+            nc.sync.dma_start(out=out_view[:, stripes, P * chunk : P * (chunk + 1)], in_=rows[:])
 
         scalar, vector, gpsimd = nc.scalar, nc.vector, nc.gpsimd
 

from contextlib import ExitStack

import concourse.mybir as mybir
from concourse.masks import make_identity

F32 = mybir.dt.float32
BF16 = mybir.dt.bfloat16
U32 = mybir.dt.uint32
U8 = mybir.dt.uint8
FP8X4 = mybir.dt.float8_e4m3fn_x4
ALU = mybir.AluOpType
ACT = mybir.ActivationFunctionType

P = 128
ROWS = 1024
WIDTH = 512
PACK = 4
STRIPES = ROWS // P
PIECE = 256
HALF = 512
HALVES = ROWS // HALF
W1_PART = 256
RUN = 4
BN_STATS_SIZE = 6
BANKS = 8
EPS = 1e-5
SLOPE = 0.01

FLOPS = 2 * 2 * ROWS * WIDTH * WIDTH


def tile_attention_prop_pa_kernel(tc, x, w1, b1, w2, b2, gamma, beta, out):
    nc = tc.nc
    with ExitStack() as ctx:
        sbuf = ctx.enter_context(tc.tile_pool(name="sbuf", bufs=1))
        psum = ctx.enter_context(tc.psum_pool(name="psum", bufs=1))
        ctx.enter_context(tc.manual_schedule())

        banks_taken = [0]

        def next_bank(shape, name):
            tag = "bank%d" % (banks_taken[0] % BANKS)
            banks_taken[0] = banks_taken[0] + 1
            return psum.tile(shape, F32, tag=tag, name=name)

        b1_rows = sbuf.tile([P, P], BF16, name="b1_rows")
        nc.vector.memset(b1_rows[:], 0.0)
        rest_rows = sbuf.tile([P, P], BF16, name="rest_rows")
        nc.vector.memset(rest_rows[:], 0.0)
        one = sbuf.tile([P, 1], F32, name="one")
        nc.vector.memset(one[:], 1.0)
        nc.scalar.dma_start(out=b1_rows[0:PACK, :], in_=b1.rearrange("(t p) -> t p", p=P))
        table_warmer = sbuf.tile([P, 1], F32, name="table_warmer")
        nc.scalar.activation(out=table_warmer[:], in_=one[:], func=ACT.Abs_reciprocal_sqrt)
        identity = sbuf.tile([P, P], F32, name="identity")
        make_identity(nc, identity[:])
        for r, values in enumerate((b2, gamma, beta)):
            nc.gpsimd.dma_start(
                out=rest_rows[PACK * r : PACK * (r + 1), :], in_=values.rearrange("(t p) -> t p", p=P)
            )

        x_view = x.rearrange("(i c) k -> i (c k)", c=STRIPES)
        stripes_in_piece = PIECE // P
        x_share = stripes_in_piece * WIDTH
        w_view = {
            "w1a": w1.rearrange("(p t) f -> p t f", t=PACK)[:, :, 0:W1_PART],
            "w1b": w1.rearrange("(p t) f -> p t f", t=PACK)[:, :, W1_PART:WIDTH],
            "w2": w2.rearrange("(t p) f -> p t f", p=P),
        }
        w_width = {"w1a": W1_PART, "w1b": WIDTH - W1_PART, "w2": WIDTH}
        x_raw = {}
        w_raw = {}

        def load_x(piece):
            x_raw[piece] = sbuf.tile([P, x_share], BF16, name="x_raw%d" % piece)
            nc.sync.dma_start(out=x_raw[piece][:], in_=x_view[:, x_share * piece : x_share * (piece + 1)])

        def load_w(part):
            w_raw[part] = sbuf.tile([P, PACK, w_width[part]], BF16, name="raw_" + part)
            nc.sync.dma_start(out=w_raw[part][:], in_=w_view[part])

        load_x(0)
        load_w("w1a")
        load_x(1)
        load_w("w1b")
        load_x(2)
        load_w("w2")
        load_x(3)

        w1_words = sbuf.tile([P, WIDTH], U32, align_bytes=64, name="w1_words")
        w1_plane = sbuf.tile([P, WIDTH], U8, align_bytes=64, name="w1_plane")
        w2_words = sbuf.tile([P, WIDTH], U32, align_bytes=64, name="w2_words")
        w2_plane = sbuf.tile([P, WIDTH], U8, align_bytes=64, name="w2_plane")
        x_words = sbuf.tile([P, ROWS], U32, align_bytes=64, name="x_words")
        x_plane = sbuf.tile([P, ROWS], U8, align_bytes=64, name="x_plane")
        h1_words = sbuf.tile([P, ROWS], U32, align_bytes=64, name="h1_words")
        h1_plane = sbuf.tile([P, ROWS], U8, align_bytes=64, name="h1_plane")
        w_packed = {
            "w1a": (w1_words[:, 0:W1_PART], w1_plane[:, 0:W1_PART]),
            "w1b": (w1_words[:, W1_PART:WIDTH], w1_plane[:, W1_PART:WIDTH]),
            "w2": (w2_words[:], w2_plane[:]),
        }

        w_grouped = {}

        def regroup_w(part):
            w_grouped[part] = sbuf.tile([P, w_width[part], PACK], BF16, align_bytes=64, name="grouped_" + part)
            nc.vector.tensor_copy(
                out=w_grouped[part][:].rearrange("p (b r) t -> p b t r", r=RUN),
                in_=w_raw[part][:].rearrange("p t (b r) -> p b t r", r=RUN),
            )

        def quantise_w(part):
            words, plane = w_packed[part]
            nc.vector.quantize_mx(
                out=words.bitcast(FP8X4), scales=plane, in_=w_grouped[part][:].rearrange("p f t -> p (f t)")
            )

        x_bank = {}
        x_grouped = {}

        def transpose_x(piece):
            x_bank[piece] = next_bank([P, stripes_in_piece, 2, P], "x_bank%d" % piece)
            x_as_f32 = x_raw[piece][:].bitcast(F32).rearrange("i (c p u) -> i c u p", c=stripes_in_piece, u=2)
            for c in range(stripes_in_piece):
                for u in range(2):
                    nc.tensor.transpose(x_bank[piece][:, c, u, :], x_as_f32[:, c, u, :], identity[:])

        def copy_x(piece):
            x_grouped[piece] = sbuf.tile([P, PACK * PIECE], BF16, align_bytes=64, name="x_grouped%d" % piece)
            nc.scalar.copy(
                out=x_grouped[piece][:].bitcast(F32).rearrange("p (c i u) -> p c i u", c=stripes_in_piece, u=2),
                in_=x_bank[piece][:].rearrange("p c u i -> p c i u"),
            )

        def piece_columns(piece):
            return slice(PIECE * piece, PIECE * (piece + 1))

        def quantise_x(piece):
            cols = piece_columns(piece)
            nc.vector.quantize_mx(
                out=x_words[:, cols].bitcast(FP8X4), scales=x_plane[:, cols], in_=x_grouped[piece][:]
            )

        b1_f32 = sbuf.tile([P, P], F32, name="b1_f32")
        b1_col = sbuf.tile([P, PACK], F32, name="b1_col")
        small_bank = {}

        def cast_b1():
            nc.vector.tensor_copy(out=b1_f32[:], in_=b1_rows[:])

        def transpose_b1():
            small_bank["b1"] = next_bank([P, P], "b1_bank")
            nc.tensor.transpose(small_bank["b1"][:], b1_f32[:], identity[:])

        def copy_b1():
            nc.vector.tensor_copy(out=b1_col[:], in_=small_bank["b1"][:, 0:PACK])

        rest_f32 = sbuf.tile([P, P], F32, name="rest_f32")
        rest_col = sbuf.tile([P, 3 * PACK], F32, name="rest_col")
        b2_most = sbuf.tile([P, PACK], F32, name="b2_most")
        centre = sbuf.tile([P, PACK], F32, name="centre")
        minus_centre = sbuf.tile([P, PACK], F32, name="minus_centre")
        gamma_signed = sbuf.tile([P, PACK, 2], F32, name="gamma_signed")

        def beta_col(chunk):
            return rest_col[:, 2 * PACK + chunk : 2 * PACK + chunk + 1]

        def cast_rest():
            nc.scalar.copy(out=rest_f32[:], in_=rest_rows[:])

        def transpose_rest():
            small_bank["rest"] = next_bank([P, P], "rest_bank")
            nc.tensor.transpose(small_bank["rest"][:], rest_f32[:], identity[:])

        def derive_rest():
            nc.scalar.copy(out=rest_col[:], in_=small_bank["rest"][:, 0 : 3 * PACK])
            nc.scalar.mul(out=b2_most[:], in_=rest_col[:, 0:PACK], mul=1.0 - SLOPE)
            nc.scalar.copy(out=gamma_signed[:, :, 0], in_=rest_col[:, PACK : 2 * PACK])
            nc.scalar.mul(out=gamma_signed[:, :, 1], in_=rest_col[:, PACK : 2 * PACK], mul=-1.0)
            nc.scalar.activation(out=centre[:], in_=b2_most[:], func=ACT.Relu)
            nc.scalar.mul(out=minus_centre[:], in_=centre[:], mul=-1.0)

        l1_bank = {}
        v = {}
        h1_grouped = {}

        def layer1(piece, pair):
            cols = piece_columns(piece)
            l1_bank[piece, pair] = next_bank([P, 2, PIECE], "l1_bank%d_%d" % (piece, pair))
            for e in range(2):
                features = slice(P * (2 * pair + e), P * (2 * pair + e + 1))
                nc.tensor.matmul_mx(
                    out=l1_bank[piece, pair][:, e, :],
                    lhsT=w1_words[:, features].bitcast(FP8X4),
                    lhsT_scale=w1_plane[:, features],
                    rhs=x_words[:, cols].bitcast(FP8X4),
                    rhs_scale=x_plane[:, cols],
                    start=True,
                    stop=True,
                )

        def add_b1(piece):
            v[piece] = sbuf.tile([P, PACK, PIECE], F32, name="v%d" % piece)
            for t in range(PACK):
                nc.scalar.activation(
                    out=v[piece][:, t, :],
                    in_=l1_bank[piece, t // 2][:, t % 2, :],
                    func=ACT.Identity,
                    bias=b1_col[:, t : t + 1],
                    scale=1.0,
                )

        def leaky1(piece):
            h1_grouped[piece] = sbuf.tile([P, PIECE, PACK], BF16, align_bytes=64, name="h1_grouped%d" % piece)
            by_row = v[piece][:].rearrange("p t n -> p n t")
            nc.vector.scalar_tensor_tensor(
                out=h1_grouped[piece][:], in0=by_row, scalar=SLOPE, in1=by_row, op0=ALU.mult, op1=ALU.max
            )

        def quantise_h1(piece):
            cols = piece_columns(piece)
            nc.vector.quantize_mx(
                out=h1_words[:, cols].bitcast(FP8X4),
                scales=h1_plane[:, cols],
                in_=h1_grouped[piece][:].rearrange("p n t -> p (n t)"),
            )

        def half_columns(half):
            return slice(HALF * half, HALF * (half + 1))

        l2_bank = {}
        sloped = {}
        q = {}

        def layer2(chunk, half):
            features = slice(P * chunk, P * (chunk + 1))
            cols = half_columns(half)
            l2_bank[chunk, half] = next_bank([P, HALF], "l2_bank%d_%d" % (chunk, half))
            nc.tensor.matmul_mx(
                out=l2_bank[chunk, half][:],
                lhsT=w2_words[:, features].bitcast(FP8X4),
                lhsT_scale=w2_plane[:, features],
                rhs=h1_words[:, cols].bitcast(FP8X4),
                rhs_scale=h1_plane[:, cols],
                start=True,
                stop=True,
            )

        def slope2(chunk, half):
            sloped[chunk, half] = sbuf.tile([P, HALF], F32, name="sloped%d_%d" % (chunk, half))
            nc.scalar.mul(out=sloped[chunk, half][:], in_=l2_bank[chunk, half][:], mul=SLOPE)

        def leaky2(chunk, half, row_sum=None):
            if chunk not in q:
                q[chunk] = sbuf.tile([P, ROWS], F32, name="q%d" % chunk)
            nc.vector.scalar_tensor_tensor(
                out=q[chunk][:, half_columns(half)],
                in0=l2_bank[chunk, half][:],
                scalar=b2_most[:, chunk : chunk + 1],
                in1=sloped[chunk, half][:],
                op0=ALU.add,
                op1=ALU.max,
                accum_out=row_sum,
            )

        half_stats = {}
        moments = {}

        def stats_on_vector(chunk, half):
            if chunk not in half_stats:
                half_stats[chunk] = sbuf.tile([P, HALVES, BN_STATS_SIZE], F32, name="half_stats%d" % chunk)
            nc.vector.bn_stats(out=half_stats[chunk][:, half, :], in_=q[chunk][:, half_columns(half)])

        def moments_on_vector(chunk):
            moments[chunk] = sbuf.tile([P, 2], F32, name="moments%d" % chunk)
            nc.vector.bn_aggr(out=moments[chunk][:], in_=half_stats[chunk][:].rearrange("p h s -> p (h s)"))

        sums = sbuf.tile([P, HALVES], F32, name="sums")
        squares = sbuf.tile([P, HALVES], F32, name="squares")

        def squares_on_scalar(chunk, half):
            unused = sbuf.tile([P, HALF], BF16, name="unused%d" % half)
            nc.scalar.activation(
                out=unused[:],
                in_=q[chunk][:, half_columns(half)],
                func=ACT.Square,
                bias=minus_centre[:, chunk : chunk + 1],
                scale=1.0,
                accum_out=squares[:, half : half + 1],
            )

        def moments_on_gpsimd(chunk):
            moments[chunk] = sbuf.tile([P, 2], F32, name="moments%d" % chunk)
            work = sbuf.tile([P, 2], F32, name="moments_work")
            nc.gpsimd.tensor_scalar(
                out=moments[chunk][:, 0:1],
                in0=sums[:, 0:1],
                scalar1=sums[:, 1:2],
                scalar2=1.0 / ROWS,
                op0=ALU.add,
                op1=ALU.mult,
            )
            nc.gpsimd.tensor_scalar(
                out=work[:, 0:1],
                in0=squares[:, 0:1],
                scalar1=squares[:, 1:2],
                scalar2=1.0 / ROWS,
                op0=ALU.add,
                op1=ALU.mult,
            )
            nc.gpsimd.tensor_scalar(
                out=work[:, 1:2],
                in0=moments[chunk][:, 0:1],
                scalar1=minus_centre[:, chunk : chunk + 1],
                scalar2=0.0,
                op0=ALU.add,
                op1=ALU.add,
            )
            nc.gpsimd.tensor_scalar(
                out=moments[chunk][:, 1:2],
                in0=work[:, 1:2],
                scalar1=work[:, 1:2],
                scalar2=work[:, 0:1],
                op0=ALU.mult,
                op1=ALU.subtract,
            )

        inverse_deviation = {}
        gain = {}
        shift = {}

        def invert_deviation(chunk, variance_sign):
            inverse_deviation[chunk] = sbuf.tile([P, 1], F32, name="inverse_deviation%d" % chunk)
            nc.scalar.activation(
                out=inverse_deviation[chunk][:],
                in_=moments[chunk][:, 1:2],
                func=ACT.Abs_reciprocal_sqrt,
                bias=EPS,
                scale=variance_sign,
            )

        def gain_and_shift(chunk, engine):
            gain[chunk] = sbuf.tile([P, 2], F32, name="gain%d" % chunk)
            shift[chunk] = sbuf.tile([P, 1], F32, name="shift%d" % chunk)
            engine.tensor_scalar(
                out=gain[chunk][:],
                in0=gamma_signed[:, chunk, :],
                scalar1=inverse_deviation[chunk][:, 0:1],
                scalar2=0.0,
                op0=ALU.mult,
                op1=ALU.add,
            )
            engine.tensor_scalar(
                out=shift[chunk][:],
                in0=moments[chunk][:, 0:1],
                scalar1=gain[chunk][:, 1:2],
                scalar2=beta_col(chunk),
                op0=ALU.mult,
                op1=ALU.add,
            )

        y = {}

        def normalise(chunk, half, engine):
            if chunk not in y:
                y[chunk] = sbuf.tile([P, ROWS], F32, name="y%d" % chunk)
            cols = half_columns(half)
            if engine is nc.scalar:
                engine.activation(
                    out=y[chunk][:, cols],
                    in_=q[chunk][:, cols],
                    func=ACT.Identity,
                    bias=shift[chunk][:, 0:1],
                    scale=gain[chunk][:, 0:1],
                )
            else:
                engine.tensor_scalar(
                    out=y[chunk][:, cols],
                    in0=q[chunk][:, cols],
                    scalar1=gain[chunk][:, 0:1],
                    scalar2=shift[chunk][:, 0:1],
                    op0=ALU.mult,
                    op1=ALU.add,
                )

        out_bank = {}
        out_view = out.rearrange("(i c) f -> i c f", c=STRIPES)
        stripes_in_half = HALF // P

        def transpose_out(chunk, half):
            out_bank[chunk, half] = next_bank([P, stripes_in_half, P], "out_bank%d_%d" % (chunk, half))
            for c in range(stripes_in_half):
                first = HALF * half + P * c
                nc.tensor.transpose(out_bank[chunk, half][:, c, :], y[chunk][:, first : first + P], identity[:])

        def copy_and_store(chunk, half, engine):
            rows = sbuf.tile([P, stripes_in_half, P], F32, name="rows%d_%d" % (chunk, half))
            if engine is nc.scalar:
                engine.copy(out=rows[:], in_=out_bank[chunk, half][:])
            else:
                engine.tensor_copy(out=rows[:], in_=out_bank[chunk, half][:])
            stripes = slice(stripes_in_half * half, stripes_in_half * (half + 1))
            nc.sync.dma_start(out=out_view[:, stripes, P * chunk : P * (chunk + 1)], in_=rows[:])

        scalar, vector, gpsimd = nc.scalar, nc.vector, nc.gpsimd

        transpose_x(0)
        copy_x(0)
        regroup_w("w1a")
        quantise_x(0)
        quantise_w("w1a")
        transpose_x(1)
        copy_x(1)
        cast_b1()
        regroup_w("w1b")
        quantise_x(1)
        quantise_w("w1b")
        transpose_x(2)
        copy_x(2)
        transpose_b1()
        copy_b1()
        regroup_w("w2")
        quantise_x(2)
        quantise_w("w2")

        layer1(0, 0)
        layer1(0, 1)
        add_b1(0)
        transpose_x(3)
        copy_x(3)
        leaky1(0)
        quantise_x(3)
        quantise_h1(0)
        for piece in (1, 2, 3):
            layer1(piece, 0)
            layer1(piece, 1)
            add_b1(piece)
        leaky1(1)
        quantise_h1(1)
        leaky1(2)
        leaky1(3)
        quantise_h1(2)
        quantise_h1(3)

        cast_rest()
        layer2(0, 0)
        layer2(1, 0)
        transpose_rest()
        slope2(0, 0)
        derive_rest()
        slope2(1, 0)
        layer2(2, 0)
        slope2(2, 0)
        leaky2(0, 0)
        leaky2(1, 0, row_sum=sums[:, 0:1])
        stats_on_vector(0, 0)
        layer2(0, 1)
        layer2(1, 1)
        slope2(0, 1)
        slope2(1, 1)
        leaky2(0, 1)
        leaky2(1, 1, row_sum=sums[:, 1:2])
        stats_on_vector(0, 1)
        squares_on_scalar(1, 0)
        layer2(2, 1)
        slope2(2, 1)
        squares_on_scalar(1, 1)
        leaky2(2, 0)
        moments_on_vector(0)
        leaky2(2, 1)
        moments_on_gpsimd(1)
        invert_deviation(0, 1.0)
        gain_and_shift(0, vector)
        stats_on_vector(2, 0)
        stats_on_vector(2, 1)
        layer2(3, 0)
        slope2(3, 0)
        normalise(0, 0, scalar)
        normalise(0, 1, gpsimd)
        invert_deviation(1, -1.0)
        gain_and_shift(1, vector)
        layer2(3, 1)
        slope2(3, 1)
        normalise(1, 0, scalar)
        normalise(1, 1, gpsimd)
        moments_on_vector(2)
        leaky2(3, 0)
        leaky2(3, 1)
        invert_deviation(2, 1.0)
        gain_and_shift(2, gpsimd)
        stats_on_vector(3, 0)
        stats_on_vector(3, 1)

        for chunk in (0, 1):
            for half in (0, 1):
                transpose_out(chunk, half)
        copy_and_store(0, 0, scalar)
        copy_and_store(0, 1, scalar)
        copy_and_store(1, 0, scalar)
        normalise(2, 0, gpsimd)
        normalise(2, 1, vector)
        moments_on_vector(3)
        copy_and_store(1, 1, vector)
        invert_deviation(3, 1.0)
        gain_and_shift(3, vector)
        transpose_out(2, 0)
        transpose_out(2, 1)
        copy_and_store(2, 0, scalar)
        copy_and_store(2, 1, scalar)
        normalise(3, 0, vector)
        normalise(3, 1, vector)
        transpose_out(3, 0)
        transpose_out(3, 1)
        copy_and_store(3, 0, vector)
        copy_and_store(3, 1, scalar)
